import numpy as np
import ml_dtypes


def mxq(x, axis, fmt="e4m3"):
    dtype, down = {"e4m3": (ml_dtypes.float8_e4m3fn, 7), "e5m2": (ml_dtypes.float8_e5m2, 14)}[fmt]
    v = np.moveaxis(np.asarray(x, np.float32).astype(ml_dtypes.bfloat16).astype(np.float64), axis, -1)
    blocks = v.reshape(v.shape[:-1] + (-1, 32))
    amax = np.abs(blocks).max(-1, keepdims=True)
    byte = np.maximum(np.where(amax > 0, np.frexp(amax)[1] - 1 + 127, 0) - down, 1)
    scale = np.exp2(byte - 127.0)
    codes = (blocks / scale).astype(np.float32).astype(dtype).astype(np.float64)
    return np.moveaxis((codes * scale).reshape(v.shape), -1, axis)


WIDE = False


def mx_kscale(k):
    if not WIDE:
        return np.ones(k)
    levels = np.array([10, -10, 5, -5, 0])
    a = np.random.permutation(np.resize(levels, k // 512 * 4)).reshape(k // 512, 4)
    idx = np.arange(k)
    return np.exp2(a[idx // 512, idx % 128 // 32])


BF16 = ml_dtypes.bfloat16


def bf(x):
    return np.asarray(x, np.float32).astype(BF16)


def f64(x):
    return np.asarray(x).astype(np.float64)


B, T, N, M, A, C, Q, D = 1, 2, 4096, 128, 384, 128, 512, 1024
G = A + C
DILATION = 1.5
MIN_EXTENT = 0.5
GATE_TEMP = 3.0
FEAT_TEMP = 6.0
KEEP_W = 0.5


def l2norm(x, eps=1e-12):
    n = np.sqrt((x * x).sum(axis=-1, keepdims=True))
    return x / np.maximum(n, eps)


def setup_inputs():
    s, u = mx_kscale(G), mx_kscale(Q)
    return {
        "center": bf(np.random.standard_normal((B, T, N * 3)) * 5.0),
        "instance_affinity": bf(np.random.standard_normal((B, T, N, A)) * s[:A]),
        "motion_code": bf(np.random.standard_normal((B, T, N, C)) * s[A:]),
        "keep_score": bf(np.maximum(np.random.uniform(-0.05, 0.99, (B, T, N)), 0.0)),
        "query_box3d": bf(np.random.standard_normal((B, T, M, 7)) * 3.0),
        "query_feat": bf(np.random.standard_normal((B, T, M, Q)) * u),
        "presence_logit": bf(np.random.standard_normal((B, T, M))),
        "Wq": bf(np.random.standard_normal((D, Q)) / np.sqrt(Q) / u),
        "bq": bf(np.random.standard_normal(D) * 0.5),
        "Wg": bf(np.random.standard_normal((D, G)) / np.sqrt(G) / s),
        "bg": bf(np.random.standard_normal(D) * 0.5),
        "background_bias": bf(0.5 + 0.1 * np.random.standard_normal(1)),
    }


def reference(center, instance_affinity, motion_code, keep_score, query_box3d,
              query_feat, presence_logit, Wq, bq, Wg, bg, background_bias):
    b, t = center.shape[:2]
    centers = f64(center).reshape(b, t, -1, 3)
    qbox = f64(query_box3d)[..., :7]
    q_centers = qbox[..., :3]
    q_sizes = np.maximum(np.abs(qbox[..., 3:6]), MIN_EXTENT)

    delta = np.abs(centers[:, :, :, None, :] - q_centers[:, :, None, :, :])
    normalized = delta / (0.5 * DILATION * q_sizes[:, :, None, :, :])
    signed_distance = normalized.max(axis=-1) - 1.0
    gate_logit = np.clip(-signed_distance * GATE_TEMP, -8.0, 8.0)

    gfeat = np.concatenate([f64(instance_affinity), f64(motion_code)], axis=-1)
    gfeat = gfeat.reshape(b, t, -1, gfeat.shape[-1])
    qf = l2norm((mxq(f64(query_feat), 3, "e4m3") @ mxq(f64(Wq), 1, "e4m3").T) + f64(bq))
    gf = l2norm((mxq(gfeat, 3, "e4m3") @ mxq(f64(Wg), 1, "e4m3").T) + f64(bg))
    feature_similarity = mxq(gf, 3, "e4m3") @ mxq(qf, 3, "e4m3").transpose(0, 1, 3, 2)

    presence = f64(presence_logit)[:, :, None, :]
    ks = np.clip(f64(keep_score).reshape(b, t, -1, 1), 1e-4, 1.0 - 1e-4)
    routing_keep = np.log(ks) - np.log1p(-ks)

    fg_logits = presence + FEAT_TEMP * feature_similarity + gate_logit + KEEP_W * routing_keep
    bg_logits = np.zeros_like(fg_logits[..., :1]) + f64(background_bias)
    logits = np.concatenate([bg_logits, fg_logits], axis=-1)
    e = np.exp(logits - logits.max(axis=-1, keepdims=True))
    probs = e / e.sum(axis=-1, keepdims=True)
    return probs.reshape(b, -1, probs.shape[-1])

@@ -1,0 +1,455 @@
+from contextlib import ExitStack
+
+import concourse.mybir as mybir
+from concourse.masks import make_identity
+
+F32 = mybir.dt.float32
+BF16 = mybir.dt.bfloat16
+U32 = mybir.dt.uint32
+U8 = mybir.dt.uint8
+FP8X4 = mybir.dt.float8_e4m3fn_x4
+ALU = mybir.AluOpType
+ACT = mybir.ActivationFunctionType
+AX = mybir.AxisListType
+
+P = 128
+T = 2
+N = 4096
+M = 128
+A_W = 384
+G = 512
+D = 1024
+SB = 512
+NSB = T * N // SB
+FLOPS = 2 * (T * N * G * D + T * N * D * M + T * M * G * D)
+
+
+def tile_gaussianqueryassignment_t_kernel(
+    tc, center, instance_affinity, motion_code, keep_score, query_box3d, query_feat,
+    presence_logit, Wq, bq, Wg, bg, background_bias, out,
+):
+    nc = tc.nc
+    with ExitStack() as ctx:
+        ctx.enter_context(tc.manual_schedule())
+        const = ctx.enter_context(tc.tile_pool(name="const", bufs=1))
+        setup = ctx.enter_context(tc.tile_pool(name="setup", bufs=1))
+        xpool = ctx.enter_context(tc.tile_pool(name="xpool", bufs=5))
+        work = ctx.enter_context(tc.tile_pool(name="work", bufs=2))
+        vpool = ctx.enter_context(tc.tile_pool(name="vpool", bufs=4))
+        small = ctx.enter_context(tc.tile_pool(name="small", bufs=6))
+        epool = ctx.enter_context(tc.tile_pool(name="epool", bufs=2))
+        opool = ctx.enter_context(tc.tile_pool(name="opool", bufs=3))
+        psum = ctx.enter_context(tc.psum_pool(name="psum", bufs=1))
+
+        ident_f = const.tile([P, P], F32)
+        make_identity(nc, ident_f[:])
+        ident_b = const.tile([P, P], BF16)
+        make_identity(nc, ident_b[:])
+        neg_half = const.tile([P, 1], F32)
+        nc.vector.memset(neg_half[:], -0.5)
+
+        wq_raw = setup.tile([P, 8 * G], BF16, tag="w_raw", bufs=2)
+        nc.sync.dma_start(
+            out=wq_raw[:].rearrange("p (a k) -> p a k", k=G),
+            in_=Wq.rearrange("(a p) k -> p a k", p=P),
+        )
+        wg_raw = setup.tile([P, 8 * G], BF16, tag="w_raw", bufs=2)
+        nc.sync.dma_start(
+            out=wg_raw[:].rearrange("p (a k) -> p a k", k=G),
+            in_=Wg.rearrange("(a p) k -> p a k", p=P),
+        )
+        q_raw = setup.tile([P, T * G], BF16)
+        nc.scalar.dma_start(
+            out=q_raw[:].rearrange("p (t k) -> p t k", k=G),
+            in_=query_feat[0].rearrange("t m k -> m t k"),
+        )
+        bg_b = const.tile([P, D], BF16)
+        nc.scalar.dma_start(out=bg_b[:], in_=bg.partition_broadcast(P))
+        bq_b = const.tile([P, D], BF16)
+        nc.scalar.dma_start(out=bq_b[:], in_=bq.partition_broadcast(P))
+        misc = setup.tile([P, P], BF16)
+        nc.vector.memset(misc[:], 0.0)
+        nc.scalar.dma_start(
+            out=misc[0:64, :], in_=keep_score[0].rearrange("t (b p) -> (t b) p", p=P)
+        )
+        nc.scalar.dma_start(out=misc[64:66, :], in_=presence_logit[0])
+        pres_b = setup.tile([P, T * M], BF16)
+        nc.scalar.dma_start(
+            out=pres_b[:], in_=presence_logit[0].rearrange("t m -> (t m)").partition_broadcast(P)
+        )
+        box = setup.tile([P, T, 7], BF16)
+        nc.scalar.dma_start(out=box[:], in_=query_box3d[0].rearrange("t m c -> m t c"))
+        bgb = setup.tile([P, 1], BF16)
+        nc.scalar.dma_start(out=bgb[:], in_=background_bias.partition_broadcast(P))
+
+        def copy_out(which, out_ap, in_ap):
+            if which == 0:
+                nc.vector.tensor_copy(out=out_ap, in_=in_ap)
+            else:
+                nc.scalar.copy(out=out_ap, in_=in_ap)
+
+        def word_transposes(words, b0):
+            xt = psum.tile([P, 2, 2, P], F32, tag="t0")
+            for b in range(2):
+                for u in range(2):
+                    c0 = (b0 + b) * 256 + P * u
+                    nc.tensor.transpose(xt[:, b, u, :], words[:, c0:c0 + P], ident_f[:])
+            return xt
+
+        def word_copy(which, grouped, b0, xt):
+            g32 = grouped[:].bitcast(F32).rearrange("p (b r u) -> p b r u", r=P, u=2)
+            copy_out(which, g32[:, b0:b0 + 2], xt[:].rearrange("p b u r -> p b r u"))
+
+        w_codes = {}
+        w_scales = {}
+        for name, raw in (("q", wq_raw), ("g", wg_raw)):
+            grouped_w = setup.tile([P, 8 * G], BF16, align_bytes=64, tag="g0w")
+            for b0 in range(0, 8, 2):
+                xt = word_transposes(raw[:].bitcast(F32), b0)
+                word_copy((b0 // 2) % 2, grouped_w, b0, xt)
+            w_codes[name] = const.tile([P, D], U32, align_bytes=64, name="w_codes_" + name)
+            w_scales[name] = const.tile([P, D], U8, align_bytes=64, name="w_scales_" + name)
+            nc.vector.quantize_mx(
+                out=w_codes[name][:].bitcast(FP8X4), scales=w_scales[name][:], in_=grouped_w[:]
+            )
+        q_codes = const.tile([P, 2 * T * M], U32, align_bytes=64)
+        q_scales = const.tile([P, 2 * T * M], U8, align_bytes=64)
+
+        size = setup.tile([P, T, 3], F32)
+        nc.vector.scalar_tensor_tensor(
+            out=size[:], in0=box[:, :, 3:6], scalar=-1.0, in1=box[:, :, 3:6], op0=ALU.mult, op1=ALU.max
+        )
+        nc.vector.tensor_scalar(out=size[:], in0=size[:], scalar1=0.5, scalar2=1.5, op0=ALU.max, op1=ALU.mult)
+        a6 = const.tile([P, T, 3], F32)
+        nc.vector.reciprocal(out=a6[:], in_=size[:])
+        nqa6 = const.tile([P, T, 3], F32)
+        nc.vector.scalar_tensor_tensor(
+            out=nqa6[:], in0=box[:, :, 0:3], scalar=-1.0, in1=a6[:], op0=ALU.mult, op1=ALU.mult
+        )
+        pmax = setup.tile([P, T], F32)
+        nc.vector.tensor_reduce(
+            out=pmax[:], in_=pres_b[:].rearrange("p (t m) -> p t m", m=M), axis=AX.X, op=ALU.max
+        )
+        misc_t = psum.tile([P, P], BF16, tag="t0")
+        nc.tensor.transpose(misc_t[:], misc[:], ident_b[:])
+        bias_p = const.tile([P, T], F32)
+        nc.vector.scalar_tensor_tensor(
+            out=bias_p[:], in0=misc_t[:, 64:66], scalar=-6.0, in1=pmax[:], op0=ALU.add, op1=ALU.subtract
+        )
+        ks = setup.tile([P, 64], F32)
+        nc.vector.tensor_scalar(
+            out=ks[:], in0=misc_t[:, 0:64], scalar1=1e-4, scalar2=1.0 - 1e-4, op0=ALU.max, op1=ALU.min
+        )
+        l1 = setup.tile([P, 64], F32)
+        nc.scalar.activation(out=l1[:], in_=ks[:], func=ACT.Ln)
+        l2 = setup.tile([P, 64], F32)
+        nc.scalar.activation(out=l2[:], in_=ks[:], func=ACT.Ln, scale=-1.0, bias=1.0)
+        dl = setup.tile([P, 64], F32)
+        nc.vector.tensor_tensor(out=dl[:], in0=l1[:], in1=l2[:], op=ALU.subtract)
+        bgb9 = setup.tile([P, 1], F32)
+        nc.vector.tensor_scalar_add(out=bgb9[:], in0=bgb[:], scalar1=-9.0)
+        cb = setup.tile([P, T], F32)
+        nc.vector.tensor_scalar(
+            out=cb[:], in0=pmax[:], scalar1=-1.0, scalar2=bgb9[:, 0:1], op0=ALU.mult, op1=ALU.add
+        )
+        lb = setup.tile([P, 64], F32)
+        for t in range(T):
+            nc.vector.tensor_scalar(
+                out=lb[:, 32 * t:32 * t + 32], in0=dl[:, 32 * t:32 * t + 32],
+                scalar1=-0.5, scalar2=cb[:, t:t + 1], op0=ALU.mult, op1=ALU.add,
+            )
+        lneg = setup.tile([P, 64], F32)
+        nc.vector.tensor_scalar_min(out=lneg[:], in0=lb[:], scalar1=0.0)
+        lpos = setup.tile([P, 64], F32)
+        nc.vector.tensor_scalar(out=lpos[:], in0=lb[:], scalar1=-1.0, scalar2=0.0, op0=ALU.mult, op1=ALU.min)
+        ebg = const.tile([P, 64], F32)
+        nc.scalar.activation(out=ebg[:], in_=lneg[:], func=ACT.Exp)
+        ffg = const.tile([P, 64], F32)
+        nc.scalar.activation(out=ffg[:], in_=lpos[:], func=ACT.Exp)
+
+
+        widths = [T] + [4] * NSB
+        first_of = {}
+        last_of = {}
+        blocks = []
+        for g, nb in enumerate(widths):
+            first_of[len(blocks)] = g
+            for b in range(nb):
+                blocks.append((g, b))
+            last_of[len(blocks) - 1] = g
+        nblocks = len(blocks)
+
+        words = {0: q_raw[:].bitcast(F32)}
+        cens = {}
+        xts = {}
+        g0s = {}
+        codes0 = {}
+        scales0 = {}
+        us = {}
+        vs = {}
+        sss = {}
+        gfbs = {}
+        t1s = {}
+        g2s = {}
+        codes2 = {0: q_codes}
+        scales2 = {0: q_scales}
+        dists = {}
+        m2s = {}
+        sims = {}
+        ys = {}
+        es = {}
+        ets = {}
+
+        def frame_of(g):
+            return (g - 1) // (NSB // T)
+
+        def load_x(g):
+            t = frame_of(g)
+            n0 = SB * ((g - 1) % (NSB // T))
+            x = xpool.tile([P, 4 * G], BF16, tag="x")
+            xv = x[:].rearrange("p (b k) -> p b k", k=G)
+            nc.sync.dma_start(
+                out=xv[:, :, 0:A_W],
+                in_=instance_affinity[0, t, n0:n0 + SB, :].rearrange("(b p) k -> p b k", p=P),
+            )
+            nc.sync.dma_start(
+                out=xv[:, :, A_W:G],
+                in_=motion_code[0, t, n0:n0 + SB, :].rearrange("(b p) k -> p b k", p=P),
+            )
+            words[g] = x[:].bitcast(F32)
+
+        def load_cen(g):
+            t = frame_of(g)
+            n0 = SB * ((g - 1) % (NSB // T))
+            cen = epool.tile([P, 3 * SB], BF16, tag="cen", bufs=3)
+            nc.sync.dma_start(out=cen[:], in_=center[0, t, 3 * n0:3 * n0 + 3 * SB].partition_broadcast(P))
+            cens[g] = cen
+
+        def t0(g, half):
+            xts[g] = word_transposes(words[g], 2 * half)
+
+        def t0_evac(g, half):
+            if half == 0:
+                grouped = work.tile([P, widths[g] * G], BF16, align_bytes=64, tag="g0")
+                g0s[g] = grouped
+            word_copy(1, g0s[g], 2 * half, xts[g])
+
+        def q0(g):
+            codes = work.tile([P, widths[g] * P], U32, align_bytes=64, tag="codes0", bufs=3)
+            scales = work.tile([P, widths[g] * P], U8, align_bytes=64, tag="scales0", bufs=3)
+            nc.vector.quantize_mx(out=codes[:].bitcast(FP8X4), scales=scales[:], in_=g0s[g][:])
+            codes0[g] = codes
+            scales0[g] = scales
+
+        def s1(j):
+            g, b = blocks[j]
+            name = "q" if g == 0 else "g"
+            cols = slice(P * b, P * b + P)
+            us[j] = []
+            for h in range(2):
+                dcols = slice(512 * h, 512 * h + 512)
+                u = psum.tile([P, 512], F32, tag="u", bufs=4)
+                nc.tensor.matmul_mx(
+                    out=u[:],
+                    lhsT=codes0[g][:, cols].bitcast(FP8X4),
+                    lhsT_scale=scales0[g][:, cols],
+                    rhs=w_codes[name][:, dcols].bitcast(FP8X4),
+                    rhs_scale=w_scales[name][:, dcols],
+                    start=True,
+                    stop=True,
+                )
+                us[j].append(u)
+
+        def add_bias(j):
+            g, b = blocks[j]
+            bias_b = bq_b if g == 0 else bg_b
+            v = vpool.tile([P, D], F32, tag="v")
+            for h in range(2):
+                dcols = slice(512 * h, 512 * h + 512)
+                nc.vector.tensor_tensor(out=v[:, dcols], in0=us[j][h][:], in1=bias_b[:, dcols], op=ALU.add)
+            vs[j] = v
+
+        def square(j):
+            junk = work.tile([P, D], BF16, tag="junk", bufs=1)
+            ss = small.tile([P, 1], F32, tag="ss")
+            nc.scalar.activation(out=junk[:], in_=vs[j][:], func=ACT.Square, accum_out=ss[:])
+            sss[j] = ss
+
+        def normalise(j):
+            ssc = small.tile([P, 1], F32, tag="ssc")
+            nc.gpsimd.tensor_scalar(out=ssc[:], in0=sss[j][:], scalar1=1e-24, scalar2=None, op0=ALU.max)
+            rn = small.tile([P, 1], F32, tag="rn")
+            nc.gpsimd.tensor_tensor(out=rn[:], in0=ssc[:], in1=neg_half[:], op=ALU.pow)
+            gfb = work.tile([P, D], BF16, tag="gfb", bufs=3)
+            nc.gpsimd.tensor_scalar(
+                out=gfb[:], in0=vs[j][:], scalar1=rn[:, 0:1], scalar2=0.0, op0=ALU.mult, op1=ALU.add
+            )
+            gfbs[j] = gfb
+
+        def t1(j):
+            tt = psum.tile([P, 8, P], BF16, tag="t1", bufs=2)
+            for a in range(8):
+                nc.tensor.transpose(tt[:, a, :], gfbs[j][:, P * a:P * a + P], ident_b[:])
+            t1s[j] = tt
+
+        def t1_evac(j):
+            g, b = blocks[j]
+            if b == 0:
+                grouped = work.tile([P, 2, widths[g] * P, 4], BF16, align_bytes=64, tag="grouped2")
+                g2s[g] = grouped
+            which = 0 if (g > 0 and b == 1) else 1
+            copy_out(
+                which,
+                g2s[g][:, :, P * b:P * b + P, :],
+                t1s[j][:].rearrange("p (g t) n -> p g n t", t=4),
+            )
+
+        def q2(g):
+            if g > 0:
+                codes = work.tile([P, 2 * SB], U32, align_bytes=64, tag="codes2")
+                scales = work.tile([P, 2 * SB], U8, align_bytes=64, tag="scales2")
+                codes2[g] = codes
+                scales2[g] = scales
+            nc.vector.quantize_mx(
+                out=codes2[g][:].bitcast(FP8X4),
+                scales=scales2[g][:],
+                in_=g2s[g][:].rearrange("p g n t -> p (g n t)"),
+            )
+
+        def gate_abs(g, c):
+            t = frame_of(g)
+            if c == 0:
+                dist = epool.tile([P, 3, SB], F32, tag="dist")
+                dists[g] = dist
+            cv = cens[g][:].rearrange("p (n c) -> p n c", c=3)
+            nc.scalar.activation(
+                out=dists[g][:, c, :], in_=cv[:, :, c], func=ACT.Abs,
+                scale=a6[:, t, c:c + 1], bias=nqa6[:, t, c:c + 1],
+            )
+
+        def gate_max(g):
+            dist = dists[g]
+            m1 = epool.tile([P, SB], F32, tag="m1")
+            nc.vector.tensor_tensor(out=m1[:], in0=dist[:, 0, :], in1=dist[:, 1, :], op=ALU.max)
+            m2 = epool.tile([P, SB], F32, tag="m2")
+            nc.vector.tensor_tensor(out=m2[:], in0=m1[:], in1=dist[:, 2, :], op=ALU.max)
+            m2s[g] = m2
+
+        def s2(g):
+            t = frame_of(g)
+            sim = psum.tile([P, SB], F32, tag="ep")
+            for h in range(2):
+                qc = slice(h * T * M + t * M, h * T * M + t * M + M)
+                nc.tensor.matmul_mx(
+                    out=sim[:],
+                    lhsT=q_codes[:, qc].bitcast(FP8X4),
+                    lhsT_scale=q_scales[:, qc],
+                    rhs=codes2[g][:, h * SB:h * SB + SB].bitcast(FP8X4),
+                    rhs_scale=scales2[g][:, h * SB:h * SB + SB],
+                    start=(h == 0),
+                    stop=(h == 1),
+                )
+            sims[g] = sim
+
+        def logits(g):
+            y = epool.tile([P, SB], F32, tag="y")
+            nc.vector.scalar_tensor_tensor(
+                out=y[:], in0=m2s[g][:], scalar=11.0 / 6.0, in1=sims[g][:], op0=ALU.min, op1=ALU.subtract
+            )
+            ys[g] = y
+
+        def expo(g):
+            t = frame_of(g)
+            e = epool.tile([P, SB], F32, tag="e")
+            nc.scalar.activation(out=e[:], in_=ys[g][:], func=ACT.Exp, scale=-6.0, bias=bias_p[:, t:t + 1])
+            es[g] = e
+
+        def t2(g):
+            e_t = psum.tile([P, 4, P], F32, tag="ep")
+            for j in range(4):
+                nc.tensor.transpose(e_t[:, j, :], es[g][:, P * j:P * j + P], ident_f[:])
+            ets[g] = e_t
+
+        def finish(g):
+            s = g - 1
+            e_t = ets[g]
+            bc = slice(4 * s, 4 * s + 4)
+            tot = small.tile([P, 4], F32, tag="tot")
+            nc.vector.tensor_reduce(out=tot[:], in_=e_t[:], axis=AX.X, op=ALU.add)
+            nc.vector.tensor_tensor(out=tot[:], in0=tot[:], in1=ffg[:, bc], op=ALU.mult)
+            nc.vector.tensor_tensor(out=tot[:], in0=tot[:], in1=ebg[:, bc], op=ALU.add)
+            rt = small.tile([P, 4], F32, tag="rt")
+            nc.vector.reciprocal(out=rt[:], in_=tot[:])
+            sc = small.tile([P, 4], F32, tag="sc")
+            nc.vector.tensor_tensor(out=sc[:], in0=rt[:], in1=ffg[:, bc], op=ALU.mult)
+            o = opool.tile([P, 4, M + 1], F32, tag="o")
+            nc.vector.tensor_tensor(out=o[:, :, 0], in0=rt[:], in1=ebg[:, bc], op=ALU.mult)
+            nc.vector.tensor_tensor(
+                out=o[:, :, 1:M + 1], in0=e_t[:], in1=sc[:].unsqueeze(2).to_broadcast([P, 4, M]), op=ALU.mult
+            )
+            nc.sync.dma_start(
+                out=out[0, SB * s:SB * s + SB, :].rearrange("(j p) c -> p j c", p=P), in_=o[:]
+            )
+
+        def is_block(j):
+            return 0 <= j < nblocks
+
+        for tick in range(-22, nblocks + 6):
+            g = first_of.get(tick + 24)
+            if g is not None and g > 0:
+                load_x(g)
+            g = first_of.get(tick + 4)
+            if g is not None and g > 0:
+                load_cen(g)
+            if is_block(tick + 4):
+                s1(tick + 4)
+            g = last_of.get(tick - 3)
+            if g is not None and g > 0:
+                s2(g)
+            if is_block(tick + 3):
+                add_bias(tick + 3)
+            if is_block(tick + 2):
+                square(tick + 2)
+            if is_block(tick + 1):
+                normalise(tick + 1)
+            if is_block(tick):
+                t1(tick)
+            g = first_of.get(tick + 15)
+            if g is not None:
+                t0(g, 0)
+            g = first_of.get(tick + 11)
+            if g is not None and g > 0:
+                t0(g, 1)
+            g = last_of.get(tick - 5)
+            if g is not None and g > 0:
+                t2(g)
+            if is_block(tick - 1):
+                t1_evac(tick - 1)
+            g = first_of.get(tick + 14)
+            if g is not None:
+                t0_evac(g, 0)
+            g = first_of.get(tick + 10)
+            if g is not None and g > 0:
+                t0_evac(g, 1)
+            for c in range(3):
+                g = first_of.get(tick - c)
+                if g is not None and g > 0:
+                    gate_abs(g, c)
+            g = last_of.get(tick - 4)
+            if g is not None and g > 0:
+                expo(g)
+            g = last_of.get(tick - 3)
+            if g is not None and g > 0:
+                logits(g)
+            g = last_of.get(tick - 2)
+            if g is not None:
+                q2(g)
+            g = last_of.get(tick - 5)
+            if g is not None and g > 0:
+                finish(g)
+            g = first_of.get(tick - 3)
+            if g is not None and g > 0:
+                gate_max(g)
+            g = first_of.get(tick + 9)
+            if g is not None:
+                q0(g)

@@ -35,7 +35,7 @@ def tile_gaussianqueryassignment_t_kernel(
         setup = ctx.enter_context(tc.tile_pool(name="setup", bufs=1))
         xpool = ctx.enter_context(tc.tile_pool(name="xpool", bufs=5))
         work = ctx.enter_context(tc.tile_pool(name="work", bufs=2))
-        vpool = ctx.enter_context(tc.tile_pool(name="vpool", bufs=4))
+        vpool = ctx.enter_context(tc.tile_pool(name="vpool", bufs=7))
         small = ctx.enter_context(tc.tile_pool(name="small", bufs=6))
         epool = ctx.enter_context(tc.tile_pool(name="epool", bufs=2))
         opool = ctx.enter_context(tc.tile_pool(name="opool", bufs=3))
@@ -45,28 +45,14 @@ def tile_gaussianqueryassignment_t_kernel(
         make_identity(nc, ident_f[:])
         ident_b = const.tile([P, P], BF16)
         make_identity(nc, ident_b[:])
-        neg_half = const.tile([P, 1], F32)
+        neg_half = const.tile([P, 4], F32)
         nc.vector.memset(neg_half[:], -0.5)
 
-        wq_raw = setup.tile([P, 8 * G], BF16, tag="w_raw", bufs=2)
-        nc.sync.dma_start(
-            out=wq_raw[:].rearrange("p (a k) -> p a k", k=G),
-            in_=Wq.rearrange("(a p) k -> p a k", p=P),
-        )
-        wg_raw = setup.tile([P, 8 * G], BF16, tag="w_raw", bufs=2)
-        nc.sync.dma_start(
-            out=wg_raw[:].rearrange("p (a k) -> p a k", k=G),
-            in_=Wg.rearrange("(a p) k -> p a k", p=P),
-        )
         q_raw = setup.tile([P, T * G], BF16)
-        nc.scalar.dma_start(
+        nc.sync.dma_start(
             out=q_raw[:].rearrange("p (t k) -> p t k", k=G),
             in_=query_feat[0].rearrange("t m k -> m t k"),
         )
-        bg_b = const.tile([P, D], BF16)
-        nc.scalar.dma_start(out=bg_b[:], in_=bg.partition_broadcast(P))
-        bq_b = const.tile([P, D], BF16)
-        nc.scalar.dma_start(out=bq_b[:], in_=bq.partition_broadcast(P))
         misc = setup.tile([P, P], BF16)
         nc.vector.memset(misc[:], 0.0)
         nc.scalar.dma_start(
@@ -81,6 +67,10 @@ def tile_gaussianqueryassignment_t_kernel(
         nc.scalar.dma_start(out=box[:], in_=query_box3d[0].rearrange("t m c -> m t c"))
         bgb = setup.tile([P, 1], BF16)
         nc.scalar.dma_start(out=bgb[:], in_=background_bias.partition_broadcast(P))
+        bq_b = const.tile([P, D], BF16)
+        nc.scalar.dma_start(out=bq_b[:], in_=bq.partition_broadcast(P))
+        bg_b = const.tile([P, D], BF16)
+        nc.scalar.dma_start(out=bg_b[:], in_=bg.partition_broadcast(P))
 
         def copy_out(which, out_ap, in_ap):
             if which == 0:
@@ -100,72 +90,81 @@ def tile_gaussianqueryassignment_t_kernel(
             g32 = grouped[:].bitcast(F32).rearrange("p (b r u) -> p b r u", r=P, u=2)
             copy_out(which, g32[:, b0:b0 + 2], xt[:].rearrange("p b u r -> p b r u"))
 
+        w_raws = {}
         w_codes = {}
         w_scales = {}
-        for name, raw in (("q", wq_raw), ("g", wg_raw)):
-            grouped_w = setup.tile([P, 8 * G], BF16, align_bytes=64, tag="g0w")
+
+        def load_w(name, w):
+            raw = setup.tile([P, 8 * G], BF16, tag="w_raw", bufs=2)
+            nc.sync.dma_start(
+                out=raw[:].rearrange("p (a k) -> p a k", k=G), in_=w.rearrange("(a p) k -> p a k", p=P)
+            )
+            w_raws[name] = raw
+
+        def pack_w(name):
+            grouped_w = setup.tile([P, 8 * G], BF16, align_bytes=64, tag="g0w", bufs=2)
             for b0 in range(0, 8, 2):
-                xt = word_transposes(raw[:].bitcast(F32), b0)
+                xt = word_transposes(w_raws[name][:].bitcast(F32), b0)
                 word_copy((b0 // 2) % 2, grouped_w, b0, xt)
             w_codes[name] = const.tile([P, D], U32, align_bytes=64, name="w_codes_" + name)
             w_scales[name] = const.tile([P, D], U8, align_bytes=64, name="w_scales_" + name)
             nc.vector.quantize_mx(
                 out=w_codes[name][:].bitcast(FP8X4), scales=w_scales[name][:], in_=grouped_w[:]
             )
+
         q_codes = const.tile([P, 2 * T * M], U32, align_bytes=64)
         q_scales = const.tile([P, 2 * T * M], U8, align_bytes=64)
 
-        size = setup.tile([P, T, 3], F32)
-        nc.vector.scalar_tensor_tensor(
-            out=size[:], in0=box[:, :, 3:6], scalar=-1.0, in1=box[:, :, 3:6], op0=ALU.mult, op1=ALU.max
-        )
-        nc.vector.tensor_scalar(out=size[:], in0=size[:], scalar1=0.5, scalar2=1.5, op0=ALU.max, op1=ALU.mult)
         a6 = const.tile([P, T, 3], F32)
-        nc.vector.reciprocal(out=a6[:], in_=size[:])
         nqa6 = const.tile([P, T, 3], F32)
-        nc.vector.scalar_tensor_tensor(
-            out=nqa6[:], in0=box[:, :, 0:3], scalar=-1.0, in1=a6[:], op0=ALU.mult, op1=ALU.mult
-        )
-        pmax = setup.tile([P, T], F32)
-        nc.vector.tensor_reduce(
-            out=pmax[:], in_=pres_b[:].rearrange("p (t m) -> p t m", m=M), axis=AX.X, op=ALU.max
-        )
-        misc_t = psum.tile([P, P], BF16, tag="t0")
-        nc.tensor.transpose(misc_t[:], misc[:], ident_b[:])
         bias_p = const.tile([P, T], F32)
-        nc.vector.scalar_tensor_tensor(
-            out=bias_p[:], in0=misc_t[:, 64:66], scalar=-6.0, in1=pmax[:], op0=ALU.add, op1=ALU.subtract
-        )
-        ks = setup.tile([P, 64], F32)
-        nc.vector.tensor_scalar(
-            out=ks[:], in0=misc_t[:, 0:64], scalar1=1e-4, scalar2=1.0 - 1e-4, op0=ALU.max, op1=ALU.min
-        )
-        l1 = setup.tile([P, 64], F32)
-        nc.scalar.activation(out=l1[:], in_=ks[:], func=ACT.Ln)
-        l2 = setup.tile([P, 64], F32)
-        nc.scalar.activation(out=l2[:], in_=ks[:], func=ACT.Ln, scale=-1.0, bias=1.0)
-        dl = setup.tile([P, 64], F32)
-        nc.vector.tensor_tensor(out=dl[:], in0=l1[:], in1=l2[:], op=ALU.subtract)
-        bgb9 = setup.tile([P, 1], F32)
-        nc.vector.tensor_scalar_add(out=bgb9[:], in0=bgb[:], scalar1=-9.0)
-        cb = setup.tile([P, T], F32)
-        nc.vector.tensor_scalar(
-            out=cb[:], in0=pmax[:], scalar1=-1.0, scalar2=bgb9[:, 0:1], op0=ALU.mult, op1=ALU.add
-        )
-        lb = setup.tile([P, 64], F32)
-        for t in range(T):
-            nc.vector.tensor_scalar(
-                out=lb[:, 32 * t:32 * t + 32], in0=dl[:, 32 * t:32 * t + 32],
-                scalar1=-0.5, scalar2=cb[:, t:t + 1], op0=ALU.mult, op1=ALU.add,
-            )
-        lneg = setup.tile([P, 64], F32)
-        nc.vector.tensor_scalar_min(out=lneg[:], in0=lb[:], scalar1=0.0)
-        lpos = setup.tile([P, 64], F32)
-        nc.vector.tensor_scalar(out=lpos[:], in0=lb[:], scalar1=-1.0, scalar2=0.0, op0=ALU.mult, op1=ALU.min)
         ebg = const.tile([P, 64], F32)
-        nc.scalar.activation(out=ebg[:], in_=lneg[:], func=ACT.Exp)
-        ffg = const.tile([P, 64], F32)
-        nc.scalar.activation(out=ffg[:], in_=lpos[:], func=ACT.Exp)
+        pmax = setup.tile([P, T], F32)
+        l1 = setup.tile([P, 64], F32)
+        l2 = setup.tile([P, 64], F32)
+
+        def constants_a():
+            size = setup.tile([P, T, 3], F32)
+            nc.vector.scalar_tensor_tensor(
+                out=size[:], in0=box[:, :, 3:6], scalar=-1.0, in1=box[:, :, 3:6], op0=ALU.mult, op1=ALU.max
+            )
+            nc.vector.tensor_scalar(out=size[:], in0=size[:], scalar1=0.5, scalar2=1.5, op0=ALU.max, op1=ALU.mult)
+            nc.vector.reciprocal(out=a6[:], in_=size[:])
+            nc.vector.scalar_tensor_tensor(
+                out=nqa6[:], in0=box[:, :, 0:3], scalar=-1.0, in1=a6[:], op0=ALU.mult, op1=ALU.mult
+            )
+            nc.vector.tensor_reduce(
+                out=pmax[:], in_=pres_b[:].rearrange("p (t m) -> p t m", m=M), axis=AX.X, op=ALU.max
+            )
+            misc_t = psum.tile([P, P], BF16, tag="t0")
+            nc.tensor.transpose(misc_t[:], misc[:], ident_b[:])
+            nc.vector.scalar_tensor_tensor(
+                out=bias_p[:], in0=misc_t[:, 64:66], scalar=-6.0, in1=pmax[:], op0=ALU.add, op1=ALU.subtract
+            )
+            ks = setup.tile([P, 64], F32)
+            nc.vector.tensor_scalar(
+                out=ks[:], in0=misc_t[:, 0:64], scalar1=1e-4, scalar2=1.0 - 1e-4, op0=ALU.max, op1=ALU.min
+            )
+            nc.scalar.activation(out=l1[:], in_=ks[:], func=ACT.Ln)
+            nc.scalar.activation(out=l2[:], in_=ks[:], func=ACT.Ln, scale=-1.0, bias=1.0)
+
+        def constants_b():
+            dl = setup.tile([P, 64], F32)
+            nc.vector.tensor_tensor(out=dl[:], in0=l1[:], in1=l2[:], op=ALU.subtract)
+            bgb9 = setup.tile([P, 1], F32)
+            nc.vector.tensor_scalar_add(out=bgb9[:], in0=bgb[:], scalar1=-9.0)
+            cb = setup.tile([P, T], F32)
+            nc.vector.tensor_scalar(
+                out=cb[:], in0=pmax[:], scalar1=-1.0, scalar2=bgb9[:, 0:1], op0=ALU.mult, op1=ALU.add
+            )
+            lb = setup.tile([P, 64], F32)
+            for t in range(T):
+                nc.vector.tensor_scalar(
+                    out=lb[:, 32 * t:32 * t + 32], in0=dl[:, 32 * t:32 * t + 32],
+                    scalar1=-0.5, scalar2=cb[:, t:t + 1], op0=ALU.mult, op1=ALU.add,
+                )
+            nc.vector.tensor_scalar_min(out=lb[:], in0=lb[:], scalar1=80.0)
+            nc.scalar.activation(out=ebg[:], in_=lb[:], func=ACT.Exp)
 
 
         widths = [T] + [4] * NSB
@@ -189,6 +188,7 @@ def tile_gaussianqueryassignment_t_kernel(
         vs = {}
         sss = {}
         gfbs = {}
+        rns = {}
         t1s = {}
         g2s = {}
         codes2 = {0: q_codes}
@@ -232,7 +232,7 @@ def tile_gaussianqueryassignment_t_kernel(
             if half == 0:
                 grouped = work.tile([P, widths[g] * G], BF16, align_bytes=64, tag="g0")
                 g0s[g] = grouped
-            word_copy(1, g0s[g], 2 * half, xts[g])
+            word_copy(0, g0s[g], 2 * half, xts[g])
 
         def q0(g):
             codes = work.tile([P, widths[g] * P], U32, align_bytes=64, tag="codes0", bufs=3)
@@ -270,19 +270,26 @@ def tile_gaussianqueryassignment_t_kernel(
             vs[j] = v
 
         def square(j):
+            g, b = blocks[j]
+            if b == 0:
+                ss = small.tile([P, 4], F32, tag="ss", bufs=3)
+                sss[g] = ss
             junk = work.tile([P, D], BF16, tag="junk", bufs=1)
-            ss = small.tile([P, 1], F32, tag="ss")
-            nc.scalar.activation(out=junk[:], in_=vs[j][:], func=ACT.Square, accum_out=ss[:])
-            sss[j] = ss
+            nc.scalar.activation(out=junk[:], in_=vs[j][:], func=ACT.Square, accum_out=sss[g][:, b:b + 1])
 
-        def normalise(j):
-            ssc = small.tile([P, 1], F32, tag="ssc")
-            nc.gpsimd.tensor_scalar(out=ssc[:], in0=sss[j][:], scalar1=1e-24, scalar2=None, op0=ALU.max)
-            rn = small.tile([P, 1], F32, tag="rn")
-            nc.gpsimd.tensor_tensor(out=rn[:], in0=ssc[:], in1=neg_half[:], op=ALU.pow)
+        def inverse_norms(g):
+            nb = widths[g]
+            ssc = small.tile([P, 4], F32, tag="ssc", bufs=2)
+            nc.gpsimd.tensor_scalar(out=ssc[:, 0:nb], in0=sss[g][:, 0:nb], scalar1=1e-24, scalar2=None, op0=ALU.max)
+            rn = small.tile([P, 4], F32, tag="rn", bufs=3)
+            nc.gpsimd.tensor_tensor(out=rn[:, 0:nb], in0=ssc[:, 0:nb], in1=neg_half[:, 0:nb], op=ALU.pow)
+            rns[g] = rn
+
+        def scale(j):
+            g, b = blocks[j]
             gfb = work.tile([P, D], BF16, tag="gfb", bufs=3)
             nc.gpsimd.tensor_scalar(
-                out=gfb[:], in0=vs[j][:], scalar1=rn[:, 0:1], scalar2=0.0, op0=ALU.mult, op1=ALU.add
+                out=gfb[:], in0=vs[j][:], scalar1=rns[g][:, b:b + 1], scalar2=0.0, op0=ALU.mult, op1=ALU.add
             )
             gfbs[j] = gfb
 
@@ -297,9 +304,8 @@ def tile_gaussianqueryassignment_t_kernel(
             if b == 0:
                 grouped = work.tile([P, 2, widths[g] * P, 4], BF16, align_bytes=64, tag="grouped2")
                 g2s[g] = grouped
-            which = 0 if (g > 0 and b == 1) else 1
             copy_out(
-                which,
+                1,
                 g2s[g][:, :, P * b:P * b + P, :],
                 t1s[j][:].rearrange("p (g t) n -> p g n t", t=4),
             )
@@ -331,7 +337,7 @@ def tile_gaussianqueryassignment_t_kernel(
             dist = dists[g]
             m1 = epool.tile([P, SB], F32, tag="m1")
             nc.vector.tensor_tensor(out=m1[:], in0=dist[:, 0, :], in1=dist[:, 1, :], op=ALU.max)
-            m2 = epool.tile([P, SB], F32, tag="m2")
+            m2 = epool.tile([P, SB], F32, tag="m2", bufs=3)
             nc.vector.tensor_tensor(out=m2[:], in0=m1[:], in1=dist[:, 2, :], op=ALU.max)
             m2s[g] = m2
 
@@ -376,16 +382,13 @@ def tile_gaussianqueryassignment_t_kernel(
             bc = slice(4 * s, 4 * s + 4)
             tot = small.tile([P, 4], F32, tag="tot")
             nc.vector.tensor_reduce(out=tot[:], in_=e_t[:], axis=AX.X, op=ALU.add)
-            nc.vector.tensor_tensor(out=tot[:], in0=tot[:], in1=ffg[:, bc], op=ALU.mult)
             nc.vector.tensor_tensor(out=tot[:], in0=tot[:], in1=ebg[:, bc], op=ALU.add)
             rt = small.tile([P, 4], F32, tag="rt")
             nc.vector.reciprocal(out=rt[:], in_=tot[:])
-            sc = small.tile([P, 4], F32, tag="sc")
-            nc.vector.tensor_tensor(out=sc[:], in0=rt[:], in1=ffg[:, bc], op=ALU.mult)
             o = opool.tile([P, 4, M + 1], F32, tag="o")
             nc.vector.tensor_tensor(out=o[:, :, 0], in0=rt[:], in1=ebg[:, bc], op=ALU.mult)
             nc.vector.tensor_tensor(
-                out=o[:, :, 1:M + 1], in0=e_t[:], in1=sc[:].unsqueeze(2).to_broadcast([P, 4, M]), op=ALU.mult
+                out=o[:, :, 1:M + 1], in0=e_t[:], in1=rt[:].unsqueeze(2).to_broadcast([P, 4, M]), op=ALU.mult
             )
             nc.sync.dma_start(
                 out=out[0, SB * s:SB * s + SB, :].rearrange("(j p) c -> p j c", p=P), in_=o[:]
@@ -394,62 +397,80 @@ def tile_gaussianqueryassignment_t_kernel(
         def is_block(j):
             return 0 <= j < nblocks
 
-        for tick in range(-22, nblocks + 6):
-            g = first_of.get(tick + 24)
-            if g is not None and g > 0:
+        def group(table, key):
+            g = table.get(key)
+            return g if (g is not None and g > 0) else None
+
+        load_w("q", Wq)
+        for tick in range(-24, nblocks + 6):
+            g = group(first_of, tick + 26)
+            if g is not None:
                 load_x(g)
-            g = first_of.get(tick + 4)
-            if g is not None and g > 0:
+            if tick == -23:
+                load_w("g", Wg)
+            g = group(first_of, tick + 8)
+            if g is not None:
                 load_cen(g)
-            if is_block(tick + 4):
-                s1(tick + 4)
-            g = last_of.get(tick - 3)
-            if g is not None and g > 0:
+            if tick == -15:
+                constants_a()
+            if tick == -3:
+                constants_b()
+            if is_block(tick + 7):
+                s1(tick + 7)
+            g = group(last_of, tick - 3)
+            if g is not None:
                 s2(g)
-            if is_block(tick + 3):
-                add_bias(tick + 3)
-            if is_block(tick + 2):
-                square(tick + 2)
+            if is_block(tick + 6):
+                add_bias(tick + 6)
+            if is_block(tick + 5):
+                square(tick + 5)
+            g = first_of.get(tick + 1)
+            if g is not None:
+                inverse_norms(g)
             if is_block(tick + 1):
-                normalise(tick + 1)
+                scale(tick + 1)
             if is_block(tick):
                 t1(tick)
-            g = first_of.get(tick + 15)
+            g = first_of.get(tick + 14)
             if g is not None:
                 t0(g, 0)
-            g = first_of.get(tick + 11)
-            if g is not None and g > 0:
+            g = group(first_of, tick + 12)
+            if g is not None:
                 t0(g, 1)
-            g = last_of.get(tick - 5)
-            if g is not None and g > 0:
+            g = group(last_of, tick - 5)
+            if g is not None:
                 t2(g)
             if is_block(tick - 1):
                 t1_evac(tick - 1)
-            g = first_of.get(tick + 14)
+            for c in range(3):
+                g = group(first_of, tick - c)
+                if g is not None:
+                    gate_abs(g, c)
+            g = group(last_of, tick - 4)
+            if g is not None:
+                expo(g)
+            g = first_of.get(tick + 13)
             if g is not None:
                 t0_evac(g, 0)
-            g = first_of.get(tick + 10)
-            if g is not None and g > 0:
+            g = group(first_of, tick + 11)
+            if g is not None:
                 t0_evac(g, 1)
-            for c in range(3):
-                g = first_of.get(tick - c)
-                if g is not None and g > 0:
-                    gate_abs(g, c)
-            g = last_of.get(tick - 4)
-            if g is not None and g > 0:
-                expo(g)
-            g = last_of.get(tick - 3)
-            if g is not None and g > 0:
+            g = group(last_of, tick - 3)
+            if g is not None:
                 logits(g)
             g = last_of.get(tick - 2)
             if g is not None:
                 q2(g)
-            g = last_of.get(tick - 5)
-            if g is not None and g > 0:
+            g = group(last_of, tick - 5)
+            if g is not None:
                 finish(g)
-            g = first_of.get(tick - 3)
-            if g is not None and g > 0:
+            g = group(first_of, tick - 3)
+            if g is not None:
                 gate_max(g)
-            g = first_of.get(tick + 9)
+            g = first_of.get(tick + 10)
             if g is not None:
                 q0(g)
+            if tick == -13:
+                pack_w("q")
+            if tick == -11:
+                pack_w("g")

@@ -241,14 +241,13 @@ def tile_gaussianqueryassignment_t_kernel(
             codes0[g] = codes
             scales0[g] = scales
 
-        def s1(j):
+        def s1(j, h):
             g, b = blocks[j]
             name = "q" if g == 0 else "g"
             cols = slice(P * b, P * b + P)
-            us[j] = []
-            for h in range(2):
-                dcols = slice(512 * h, 512 * h + 512)
-                u = psum.tile([P, 512], F32, tag="u", bufs=4)
+            dcols = slice(512 * h, 512 * h + 512)
+            u = psum.tile([P, 512], F32, tag="u", bufs=4)
+            for again in range(2):
                 nc.tensor.matmul_mx(
                     out=u[:],
                     lhsT=codes0[g][:, cols].bitcast(FP8X4),
@@ -258,7 +257,9 @@ def tile_gaussianqueryassignment_t_kernel(
                     start=True,
                     stop=True,
                 )
-                us[j].append(u)
+            if h == 0:
+                us[j] = []
+            us[j].append(u)
 
         def add_bias(j):
             g, b = blocks[j]
@@ -416,7 +417,7 @@ def tile_gaussianqueryassignment_t_kernel(
             if tick == -3:
                 constants_b()
             if is_block(tick + 7):
-                s1(tick + 7)
+                s1(tick + 7, 0)
             g = group(last_of, tick - 3)
             if g is not None:
                 s2(g)
@@ -431,6 +432,8 @@ def tile_gaussianqueryassignment_t_kernel(
                 scale(tick + 1)
             if is_block(tick):
                 t1(tick)
+            if is_block(tick + 7):
+                s1(tick + 7, 1)
             g = first_of.get(tick + 14)
             if g is not None:
                 t0(g, 0)

@@ -21,6 +21,7 @@ G = 512
 D = 1024
 SB = 512
 NSB = T * N // SB
+POOL_SCALES = (0, 1)
 FLOPS = 2 * (T * N * G * D + T * N * D * M + T * M * G * D)
 
 
@@ -35,7 +36,7 @@ def tile_gaussianqueryassignment_t_kernel(
         setup = ctx.enter_context(tc.tile_pool(name="setup", bufs=1))
         xpool = ctx.enter_context(tc.tile_pool(name="xpool", bufs=5))
         work = ctx.enter_context(tc.tile_pool(name="work", bufs=2))
-        vpool = ctx.enter_context(tc.tile_pool(name="vpool", bufs=7))
+        vpool = ctx.enter_context(tc.tile_pool(name="vpool", bufs=8))
         small = ctx.enter_context(tc.tile_pool(name="small", bufs=6))
         epool = ctx.enter_context(tc.tile_pool(name="epool", bufs=2))
         opool = ctx.enter_context(tc.tile_pool(name="opool", bufs=3))
@@ -232,7 +233,7 @@ def tile_gaussianqueryassignment_t_kernel(
             if half == 0:
                 grouped = work.tile([P, widths[g] * G], BF16, align_bytes=64, tag="g0")
                 g0s[g] = grouped
-            word_copy(0, g0s[g], 2 * half, xts[g])
+            word_copy(1 - half, g0s[g], 2 * half, xts[g])
 
         def q0(g):
             codes = work.tile([P, widths[g] * P], U32, align_bytes=64, tag="codes0", bufs=3)
@@ -241,13 +242,14 @@ def tile_gaussianqueryassignment_t_kernel(
             codes0[g] = codes
             scales0[g] = scales
 
-        def s1(j, h):
+        def s1(j):
             g, b = blocks[j]
             name = "q" if g == 0 else "g"
             cols = slice(P * b, P * b + P)
-            dcols = slice(512 * h, 512 * h + 512)
-            u = psum.tile([P, 512], F32, tag="u", bufs=4)
-            for again in range(2):
+            us[j] = []
+            for h in range(2):
+                dcols = slice(512 * h, 512 * h + 512)
+                u = psum.tile([P, 512], F32, tag="u", bufs=4)
                 nc.tensor.matmul_mx(
                     out=u[:],
                     lhsT=codes0[g][:, cols].bitcast(FP8X4),
@@ -257,9 +259,7 @@ def tile_gaussianqueryassignment_t_kernel(
                     start=True,
                     stop=True,
                 )
-            if h == 0:
-                us[j] = []
-            us[j].append(u)
+                us[j].append(u)
 
         def add_bias(j):
             g, b = blocks[j]
@@ -288,10 +288,15 @@ def tile_gaussianqueryassignment_t_kernel(
 
         def scale(j):
             g, b = blocks[j]
-            gfb = work.tile([P, D], BF16, tag="gfb", bufs=3)
-            nc.gpsimd.tensor_scalar(
-                out=gfb[:], in0=vs[j][:], scalar1=rns[g][:, b:b + 1], scalar2=0.0, op0=ALU.mult, op1=ALU.add
-            )
+            gfb = work.tile([P, D], BF16, tag="gfb", bufs=4)
+            if b in POOL_SCALES:
+                nc.gpsimd.tensor_scalar(
+                    out=gfb[:], in0=vs[j][:], scalar1=rns[g][:, b:b + 1], scalar2=0.0, op0=ALU.mult, op1=ALU.add
+                )
+            else:
+                nc.vector.tensor_scalar(
+                    out=gfb[:], in0=vs[j][:], scalar1=rns[g][:, b:b + 1], scalar2=None, op0=ALU.mult
+                )
             gfbs[j] = gfb
 
         def t1(j):
@@ -412,32 +417,32 @@ def tile_gaussianqueryassignment_t_kernel(
             g = group(first_of, tick + 8)
             if g is not None:
                 load_cen(g)
-            if tick == -15:
+            if tick == -14:
                 constants_a()
             if tick == -3:
                 constants_b()
-            if is_block(tick + 7):
-                s1(tick + 7, 0)
+            if is_block(tick + 8):
+                s1(tick + 8)
             g = group(last_of, tick - 3)
             if g is not None:
                 s2(g)
+            if is_block(tick + 7):
+                add_bias(tick + 7)
             if is_block(tick + 6):
-                add_bias(tick + 6)
-            if is_block(tick + 5):
-                square(tick + 5)
-            g = first_of.get(tick + 1)
+                square(tick + 6)
+            g = first_of.get(tick + 2)
             if g is not None:
                 inverse_norms(g)
-            if is_block(tick + 1):
+            if is_block(tick + 2) and blocks[tick + 2][1] in POOL_SCALES:
+                scale(tick + 2)
+            if is_block(tick + 1) and blocks[tick + 1][1] not in POOL_SCALES:
                 scale(tick + 1)
             if is_block(tick):
                 t1(tick)
-            if is_block(tick + 7):
-                s1(tick + 7, 1)
-            g = first_of.get(tick + 14)
+            g = first_of.get(tick + 13)
             if g is not None:
                 t0(g, 0)
-            g = group(first_of, tick + 12)
+            g = group(first_of, tick + 11)
             if g is not None:
                 t0(g, 1)
             g = group(last_of, tick - 5)
@@ -445,6 +450,9 @@ def tile_gaussianqueryassignment_t_kernel(
                 t2(g)
             if is_block(tick - 1):
                 t1_evac(tick - 1)
+            g = first_of.get(tick + 12)
+            if g is not None:
+                t0_evac(g, 0)
             for c in range(3):
                 g = group(first_of, tick - c)
                 if g is not None:
@@ -452,10 +460,7 @@ def tile_gaussianqueryassignment_t_kernel(
             g = group(last_of, tick - 4)
             if g is not None:
                 expo(g)
-            g = first_of.get(tick + 13)
-            if g is not None:
-                t0_evac(g, 0)
-            g = group(first_of, tick + 11)
+            g = group(first_of, tick + 10)
             if g is not None:
                 t0_evac(g, 1)
             g = group(last_of, tick - 3)
@@ -470,10 +475,10 @@ def tile_gaussianqueryassignment_t_kernel(
             g = group(first_of, tick - 3)
             if g is not None:
                 gate_max(g)
-            g = first_of.get(tick + 10)
+            g = first_of.get(tick + 9)
             if g is not None:
                 q0(g)
-            if tick == -13:
+            if tick == -12:
                 pack_w("q")
-            if tick == -11:
+            if tick == -10:
                 pack_w("g")

@@ -21,8 +21,8 @@ G = 512
 D = 1024
 SB = 512
 NSB = T * N // SB
-POOL_SCALES = (0, 1)
 FLOPS = 2 * (T * N * G * D + T * N * D * M + T * M * G * D)
+QUERIES = 1
 
 
 def tile_gaussianqueryassignment_t_kernel(
@@ -42,6 +42,53 @@ def tile_gaussianqueryassignment_t_kernel(
         opool = ctx.enter_context(tc.tile_pool(name="opool", bufs=3))
         psum = ctx.enter_context(tc.psum_pool(name="psum", bufs=1))
 
+        widths = [4] * (NSB + 1)
+        widths[QUERIES] = T
+        blocks = []
+        first = []
+        last = []
+        for g, nb in enumerate(widths):
+            first.append(len(blocks))
+            for b in range(nb):
+                blocks.append((g, b))
+            last.append(len(blocks) - 1)
+        nblocks = len(blocks)
+
+        def sb_of(g):
+            return g if g < QUERIES else g - 1
+
+        def frame_of(g):
+            return sb_of(g) // (NSB // T)
+
+        def n0_of(g):
+            return SB * (sb_of(g) % (NSB // T))
+
+        at = {}
+        for kind in ("load_x", "load_cen", "t0a", "eva", "t0b", "evb", "q0", "rn", "abs0", "abs1", "abs2",
+                     "gmax", "q2", "s2", "exp", "t2"):
+            at[kind] = {}
+        for g, nb in enumerate(widths):
+            f = first[g]
+            e = last[g]
+            at["t0a"][f - 14] = g
+            at["eva"][f - 13] = g
+            at["q0"][f - 10] = g
+            at["rn"][f - 2] = g
+            at["q2"][e + 2] = g
+            if g != QUERIES:
+                late = 2 if g < QUERIES else 0
+                at["load_x"][f - 26] = g
+                at["load_cen"][f - 8] = g
+                at["t0b"][f - 12] = g
+                at["evb"][f - 11] = g
+                at["abs0"][f] = g
+                at["abs1"][f + 1] = g
+                at["abs2"][f + 2] = g
+                at["gmax"][f + 3] = g
+                at["s2"][e + 3 + late] = g
+                at["exp"][e + 4 + late] = g
+                at["t2"][e + 5 + late] = g
+
         ident_f = const.tile([P, P], F32)
         make_identity(nc, ident_f[:])
         ident_b = const.tile([P, P], BF16)
@@ -49,11 +96,6 @@ def tile_gaussianqueryassignment_t_kernel(
         neg_half = const.tile([P, 4], F32)
         nc.vector.memset(neg_half[:], -0.5)
 
-        q_raw = setup.tile([P, T * G], BF16)
-        nc.sync.dma_start(
-            out=q_raw[:].rearrange("p (t k) -> p t k", k=G),
-            in_=query_feat[0].rearrange("t m k -> m t k"),
-        )
         misc = setup.tile([P, P], BF16)
         nc.vector.memset(misc[:], 0.0)
         nc.scalar.dma_start(
@@ -68,10 +110,11 @@ def tile_gaussianqueryassignment_t_kernel(
         nc.scalar.dma_start(out=box[:], in_=query_box3d[0].rearrange("t m c -> m t c"))
         bgb = setup.tile([P, 1], BF16)
         nc.scalar.dma_start(out=bgb[:], in_=background_bias.partition_broadcast(P))
-        bq_b = const.tile([P, D], BF16)
-        nc.scalar.dma_start(out=bq_b[:], in_=bq.partition_broadcast(P))
         bg_b = const.tile([P, D], BF16)
         nc.scalar.dma_start(out=bg_b[:], in_=bg.partition_broadcast(P))
+        bq_b = const.tile([P, D], BF16)
+        nc.scalar.dma_start(out=bq_b[:], in_=bq.partition_broadcast(P))
+        q_raw = setup.tile([P, T * G], BF16)
 
         def copy_out(which, out_ap, in_ap):
             if which == 0:
@@ -79,8 +122,8 @@ def tile_gaussianqueryassignment_t_kernel(
             else:
                 nc.scalar.copy(out=out_ap, in_=in_ap)
 
-        def word_transposes(words, b0):
-            xt = psum.tile([P, 2, 2, P], F32, tag="t0")
+        def word_transposes(words, b0, tag, bufs):
+            xt = psum.tile([P, 2, 2, P], F32, tag=tag, bufs=bufs)
             for b in range(2):
                 for u in range(2):
                     c0 = (b0 + b) * 256 + P * u
@@ -97,21 +140,24 @@ def tile_gaussianqueryassignment_t_kernel(
 
         def load_w(name, w):
             raw = setup.tile([P, 8 * G], BF16, tag="w_raw", bufs=2)
-            nc.sync.dma_start(
-                out=raw[:].rearrange("p (a k) -> p a k", k=G), in_=w.rearrange("(a p) k -> p a k", p=P)
-            )
+            rv = raw[:].rearrange("p (a k) -> p a k", k=G)
+            wv = w.rearrange("(a p) k -> p a k", p=P)
+            for h in range(2):
+                nc.sync.dma_start(out=rv[:, 4 * h:4 * h + 4, :], in_=wv[:, 4 * h:4 * h + 4, :])
             w_raws[name] = raw
-
-        def pack_w(name):
-            grouped_w = setup.tile([P, 8 * G], BF16, align_bytes=64, tag="g0w", bufs=2)
-            for b0 in range(0, 8, 2):
-                xt = word_transposes(w_raws[name][:].bitcast(F32), b0)
-                word_copy((b0 // 2) % 2, grouped_w, b0, xt)
             w_codes[name] = const.tile([P, D], U32, align_bytes=64, name="w_codes_" + name)
             w_scales[name] = const.tile([P, D], U8, align_bytes=64, name="w_scales_" + name)
-            nc.vector.quantize_mx(
-                out=w_codes[name][:].bitcast(FP8X4), scales=w_scales[name][:], in_=grouped_w[:]
-            )
+
+        def pack_w(name, tag, bufs):
+            for h in range(2):
+                grouped_w = setup.tile([P, 4 * G], BF16, align_bytes=64, tag="g0w", bufs=2)
+                for i in range(2):
+                    xt = word_transposes(w_raws[name][:].bitcast(F32), 4 * h + 2 * i, tag, bufs)
+                    word_copy(i, grouped_w, 2 * i, xt)
+                dcols = slice(512 * h, 512 * h + 512)
+                nc.vector.quantize_mx(
+                    out=w_codes[name][:, dcols].bitcast(FP8X4), scales=w_scales[name][:, dcols], in_=grouped_w[:]
+                )
 
         q_codes = const.tile([P, 2 * T * M], U32, align_bytes=64)
         q_scales = const.tile([P, 2 * T * M], U8, align_bytes=64)
@@ -121,6 +167,7 @@ def tile_gaussianqueryassignment_t_kernel(
         bias_p = const.tile([P, T], F32)
         ebg = const.tile([P, 64], F32)
         pmax = setup.tile([P, T], F32)
+        ks = setup.tile([P, 64], F32)
         l1 = setup.tile([P, 64], F32)
         l2 = setup.tile([P, 64], F32)
 
@@ -142,10 +189,11 @@ def tile_gaussianqueryassignment_t_kernel(
             nc.vector.scalar_tensor_tensor(
                 out=bias_p[:], in0=misc_t[:, 64:66], scalar=-6.0, in1=pmax[:], op0=ALU.add, op1=ALU.subtract
             )
-            ks = setup.tile([P, 64], F32)
             nc.vector.tensor_scalar(
                 out=ks[:], in0=misc_t[:, 0:64], scalar1=1e-4, scalar2=1.0 - 1e-4, op0=ALU.max, op1=ALU.min
             )
+
+        def constants_ln():
             nc.scalar.activation(out=l1[:], in_=ks[:], func=ACT.Ln)
             nc.scalar.activation(out=l2[:], in_=ks[:], func=ACT.Ln, scale=-1.0, bias=1.0)
 
@@ -167,19 +215,7 @@ def tile_gaussianqueryassignment_t_kernel(
             nc.vector.tensor_scalar_min(out=lb[:], in0=lb[:], scalar1=80.0)
             nc.scalar.activation(out=ebg[:], in_=lb[:], func=ACT.Exp)
 
-
-        widths = [T] + [4] * NSB
-        first_of = {}
-        last_of = {}
-        blocks = []
-        for g, nb in enumerate(widths):
-            first_of[len(blocks)] = g
-            for b in range(nb):
-                blocks.append((g, b))
-            last_of[len(blocks) - 1] = g
-        nblocks = len(blocks)
-
-        words = {0: q_raw[:].bitcast(F32)}
+        words = {QUERIES: q_raw[:].bitcast(F32)}
         cens = {}
         xts = {}
         g0s = {}
@@ -188,12 +224,12 @@ def tile_gaussianqueryassignment_t_kernel(
         us = {}
         vs = {}
         sss = {}
-        gfbs = {}
         rns = {}
+        gfbs = {}
         t1s = {}
         g2s = {}
-        codes2 = {0: q_codes}
-        scales2 = {0: q_scales}
+        codes2 = {QUERIES: q_codes}
+        scales2 = {QUERIES: q_scales}
         dists = {}
         m2s = {}
         sims = {}
@@ -201,12 +237,9 @@ def tile_gaussianqueryassignment_t_kernel(
         es = {}
         ets = {}
 
-        def frame_of(g):
-            return (g - 1) // (NSB // T)
-
         def load_x(g):
             t = frame_of(g)
-            n0 = SB * ((g - 1) % (NSB // T))
+            n0 = n0_of(g)
             x = xpool.tile([P, 4 * G], BF16, tag="x")
             xv = x[:].rearrange("p (b k) -> p b k", k=G)
             nc.sync.dma_start(
@@ -221,19 +254,19 @@ def tile_gaussianqueryassignment_t_kernel(
 
         def load_cen(g):
             t = frame_of(g)
-            n0 = SB * ((g - 1) % (NSB // T))
+            n0 = n0_of(g)
             cen = epool.tile([P, 3 * SB], BF16, tag="cen", bufs=3)
             nc.sync.dma_start(out=cen[:], in_=center[0, t, 3 * n0:3 * n0 + 3 * SB].partition_broadcast(P))
             cens[g] = cen
 
         def t0(g, half):
-            xts[g] = word_transposes(words[g], 2 * half)
+            xts[g] = word_transposes(words[g], 2 * half, "t0", 1)
 
         def t0_evac(g, half):
             if half == 0:
                 grouped = work.tile([P, widths[g] * G], BF16, align_bytes=64, tag="g0")
                 g0s[g] = grouped
-            word_copy(1 - half, g0s[g], 2 * half, xts[g])
+            word_copy(0, g0s[g], 2 * half, xts[g])
 
         def q0(g):
             codes = work.tile([P, widths[g] * P], U32, align_bytes=64, tag="codes0", bufs=3)
@@ -244,7 +277,7 @@ def tile_gaussianqueryassignment_t_kernel(
 
         def s1(j):
             g, b = blocks[j]
-            name = "q" if g == 0 else "g"
+            name = "q" if g == QUERIES else "g"
             cols = slice(P * b, P * b + P)
             us[j] = []
             for h in range(2):
@@ -263,7 +296,7 @@ def tile_gaussianqueryassignment_t_kernel(
 
         def add_bias(j):
             g, b = blocks[j]
-            bias_b = bq_b if g == 0 else bg_b
+            bias_b = bq_b if g == QUERIES else bg_b
             v = vpool.tile([P, D], F32, tag="v")
             for h in range(2):
                 dcols = slice(512 * h, 512 * h + 512)
@@ -289,14 +322,9 @@ def tile_gaussianqueryassignment_t_kernel(
         def scale(j):
             g, b = blocks[j]
             gfb = work.tile([P, D], BF16, tag="gfb", bufs=4)
-            if b in POOL_SCALES:
-                nc.gpsimd.tensor_scalar(
-                    out=gfb[:], in0=vs[j][:], scalar1=rns[g][:, b:b + 1], scalar2=0.0, op0=ALU.mult, op1=ALU.add
-                )
-            else:
-                nc.vector.tensor_scalar(
-                    out=gfb[:], in0=vs[j][:], scalar1=rns[g][:, b:b + 1], scalar2=None, op0=ALU.mult
-                )
+            nc.gpsimd.tensor_scalar(
+                out=gfb[:], in0=vs[j][:], scalar1=rns[g][:, b:b + 1], scalar2=0.0, op0=ALU.mult, op1=ALU.add
+            )
             gfbs[j] = gfb
 
         def t1(j):
@@ -317,7 +345,7 @@ def tile_gaussianqueryassignment_t_kernel(
             )
 
         def q2(g):
-            if g > 0:
+            if g != QUERIES:
                 codes = work.tile([P, 2 * SB], U32, align_bytes=64, tag="codes2")
                 scales = work.tile([P, 2 * SB], U8, align_bytes=64, tag="scales2")
                 codes2[g] = codes
@@ -383,7 +411,7 @@ def tile_gaussianqueryassignment_t_kernel(
             ets[g] = e_t
 
         def finish(g):
-            s = g - 1
+            s = sb_of(g)
             e_t = ets[g]
             bc = slice(4 * s, 4 * s + 4)
             tot = small.tile([P, 4], F32, tag="tot")
@@ -403,82 +431,81 @@ def tile_gaussianqueryassignment_t_kernel(
         def is_block(j):
             return 0 <= j < nblocks
 
-        def group(table, key):
-            g = table.get(key)
-            return g if (g is not None and g > 0) else None
-
-        load_w("q", Wq)
-        for tick in range(-24, nblocks + 6):
-            g = group(first_of, tick + 26)
+        for tick in range(-26, nblocks + 6):
+            g = at["load_x"].get(tick)
             if g is not None:
                 load_x(g)
-            if tick == -23:
+            if tick == -26:
                 load_w("g", Wg)
-            g = group(first_of, tick + 8)
+                nc.sync.dma_start(
+                    out=q_raw[:].rearrange("p (t k) -> p t k", k=G), in_=query_feat[0].rearrange("t m k -> m t k")
+                )
+                load_w("q", Wq)
+            g = at["load_cen"].get(tick)
             if g is not None:
                 load_cen(g)
-            if tick == -14:
+            if tick == -15:
                 constants_a()
+            if tick == -9:
+                constants_ln()
             if tick == -3:
                 constants_b()
+            g = at["t2"].get(tick)
+            if g is not None:
+                t2(g)
             if is_block(tick + 8):
                 s1(tick + 8)
-            g = group(last_of, tick - 3)
+            g = at["s2"].get(tick)
             if g is not None:
                 s2(g)
             if is_block(tick + 7):
                 add_bias(tick + 7)
-            if is_block(tick + 6):
-                square(tick + 6)
-            g = first_of.get(tick + 2)
-            if g is not None:
-                inverse_norms(g)
-            if is_block(tick + 2) and blocks[tick + 2][1] in POOL_SCALES:
-                scale(tick + 2)
-            if is_block(tick + 1) and blocks[tick + 1][1] not in POOL_SCALES:
-                scale(tick + 1)
-            if is_block(tick):
-                t1(tick)
-            g = first_of.get(tick + 13)
-            if g is not None:
-                t0(g, 0)
-            g = group(first_of, tick + 11)
-            if g is not None:
-                t0(g, 1)
-            g = group(last_of, tick - 5)
-            if g is not None:
-                t2(g)
-            if is_block(tick - 1):
-                t1_evac(tick - 1)
-            g = first_of.get(tick + 12)
-            if g is not None:
-                t0_evac(g, 0)
-            for c in range(3):
-                g = group(first_of, tick - c)
-                if g is not None:
-                    gate_abs(g, c)
-            g = group(last_of, tick - 4)
+            g = at["exp"].get(tick)
             if g is not None:
                 expo(g)
-            g = group(first_of, tick + 10)
+            if is_block(tick + 6):
+                square(tick + 6)
+            g = at["rn"].get(tick)
             if g is not None:
-                t0_evac(g, 1)
-            g = group(last_of, tick - 3)
+                inverse_norms(g)
+            if is_block(tick + 2):
+                scale(tick + 2)
+            if is_block(tick):
+                t1(tick)
+            g = at["t0a"].get(tick)
             if g is not None:
-                logits(g)
-            g = last_of.get(tick - 2)
+                t0(g, 0)
+            g = at["t0b"].get(tick)
+            if g is not None:
+                t0(g, 1)
+            if is_block(tick - 1):
+                t1_evac(tick - 1)
+            for c in range(3):
+                g = at["abs%d" % c].get(tick)
+                if g is not None:
+                    gate_abs(g, c)
+            g = at["q2"].get(tick)
             if g is not None:
                 q2(g)
-            g = group(last_of, tick - 5)
+            g = at["eva"].get(tick)
+            if g is not None:
+                t0_evac(g, 0)
+            g = at["evb"].get(tick)
+            if g is not None:
+                t0_evac(g, 1)
+            g = at["s2"].get(tick)
+            if g is not None:
+                logits(g)
+            g = at["t2"].get(tick)
             if g is not None:
                 finish(g)
-            g = group(first_of, tick - 3)
+            g = at["gmax"].get(tick)
             if g is not None:
                 gate_max(g)
-            g = first_of.get(tick + 9)
+            g = at["q0"].get(tick)
             if g is not None:
                 q0(g)
-            if tick == -12:
-                pack_w("q")
             if tick == -10:
-                pack_w("g")
+                pack_w("g", "u", 4)
+            if tick == -7:
+                pack_w("q", "t1", 2)

@@ -73,7 +73,7 @@ def tile_gaussianqueryassignment_t_kernel(
             at["t0a"][f - 14] = g
             at["eva"][f - 13] = g
             at["q0"][f - 10] = g
-            at["rn"][f - 2] = g
+            at["rn"][f - 3] = g
             at["q2"][e + 2] = g
             if g != QUERIES:
                 late = 2 if g < QUERIES else 0
@@ -225,6 +225,7 @@ def tile_gaussianqueryassignment_t_kernel(
         vs = {}
         sss = {}
         rns = {}
+        zeros = {}
         gfbs = {}
         t1s = {}
         g2s = {}
@@ -323,7 +324,8 @@ def tile_gaussianqueryassignment_t_kernel(
             g, b = blocks[j]
             gfb = work.tile([P, D], BF16, tag="gfb", bufs=4)
             nc.gpsimd.tensor_scalar(
-                out=gfb[:], in0=vs[j][:], scalar1=rns[g][:, b:b + 1], scalar2=0.0, op0=ALU.mult, op1=ALU.add
+                out=gfb[:], in0=vs[j][:], scalar1=rns[g][:, b:b + 1], scalar2=zeros[j][:, 0:1],
+                op0=ALU.mult, op1=ALU.add,
             )
             gfbs[j] = gfb
 
@@ -465,11 +467,11 @@ def tile_gaussianqueryassignment_t_kernel(
                 expo(g)
             if is_block(tick + 6):
                 square(tick + 6)
+            if is_block(tick + 2):
+                scale(tick + 2)
             g = at["rn"].get(tick)
             if g is not None:
                 inverse_norms(g)
-            if is_block(tick + 2):
-                scale(tick + 2)
             if is_block(tick):
                 t1(tick)
             g = at["t0a"].get(tick)
@@ -484,9 +486,6 @@ def tile_gaussianqueryassignment_t_kernel(
                 g = at["abs%d" % c].get(tick)
                 if g is not None:
                     gate_abs(g, c)
-            g = at["q2"].get(tick)
-            if g is not None:
-                q2(g)
             g = at["eva"].get(tick)
             if g is not None:
                 t0_evac(g, 0)
@@ -499,12 +498,19 @@ def tile_gaussianqueryassignment_t_kernel(
             g = at["t2"].get(tick)
             if g is not None:
                 finish(g)
+            g = at["q2"].get(tick)
+            if g is not None:
+                q2(g)
             g = at["gmax"].get(tick)
             if g is not None:
                 gate_max(g)
             g = at["q0"].get(tick)
             if g is not None:
                 q0(g)
+            if is_block(tick + 3):
+                zero = small.tile([P, 1], F32, tag="zero", bufs=3)
+                nc.vector.memset(zero[:], 0.0)
+                zeros[tick + 3] = zero
             if tick == -10:
                 pack_w("g", "u", 4)
             if tick == -7:

@@ -31,7 +31,6 @@ def tile_gaussianqueryassignment_t_kernel(
 ):
     nc = tc.nc
     with ExitStack() as ctx:
-        ctx.enter_context(tc.manual_schedule())
         const = ctx.enter_context(tc.tile_pool(name="const", bufs=1))
         setup = ctx.enter_context(tc.tile_pool(name="setup", bufs=1))
         xpool = ctx.enter_context(tc.tile_pool(name="xpool", bufs=5))

@@ -31,6 +31,7 @@ def tile_gaussianqueryassignment_t_kernel(
 ):
     nc = tc.nc
     with ExitStack() as ctx:
+        ctx.enter_context(tc.manual_schedule())
         const = ctx.enter_context(tc.tile_pool(name="const", bufs=1))
         setup = ctx.enter_context(tc.tile_pool(name="setup", bufs=1))
         xpool = ctx.enter_context(tc.tile_pool(name="xpool", bufs=5))
@@ -69,24 +70,24 @@ def tile_gaussianqueryassignment_t_kernel(
         for g, nb in enumerate(widths):
             f = first[g]
             e = last[g]
-            at["t0a"][f - 14] = g
-            at["eva"][f - 13] = g
-            at["q0"][f - 10] = g
+            at["t0a"][f - 15] = g
+            at["eva"][f - 14] = g
+            at["q0"][f - 9] = g
             at["rn"][f - 3] = g
-            at["q2"][e + 2] = g
+            at["q2"][e + 3] = g
             if g != QUERIES:
                 late = 2 if g < QUERIES else 0
                 at["load_x"][f - 26] = g
                 at["load_cen"][f - 8] = g
-                at["t0b"][f - 12] = g
-                at["evb"][f - 11] = g
-                at["abs0"][f] = g
-                at["abs1"][f + 1] = g
-                at["abs2"][f + 2] = g
-                at["gmax"][f + 3] = g
-                at["s2"][e + 3 + late] = g
-                at["exp"][e + 4 + late] = g
-                at["t2"][e + 5 + late] = g
+                at["t0b"][f - 13] = g
+                at["evb"][f - 12] = g
+                at["abs0"][f + 1] = g
+                at["abs1"][f + 2] = g
+                at["abs2"][f + 3] = g
+                at["gmax"][f + 4] = g
+                at["s2"][e + 4 + late] = g
+                at["exp"][e + 5 + late] = g
+                at["t2"][e + 6 + late] = g
 
         ident_f = const.tile([P, P], F32)
         make_identity(nc, ident_f[:])
@@ -432,7 +433,7 @@ def tile_gaussianqueryassignment_t_kernel(
         def is_block(j):
             return 0 <= j < nblocks
 
-        for tick in range(-26, nblocks + 6):
+        for tick in range(-26, nblocks + 7):
             g = at["load_x"].get(tick)
             if g is not None:
                 load_x(g)
@@ -445,7 +446,7 @@ def tile_gaussianqueryassignment_t_kernel(
             g = at["load_cen"].get(tick)
             if g is not None:
                 load_cen(g)
-            if tick == -15:
+            if tick == -16:
                 constants_a()
             if tick == -9:
                 constants_ln()

@@ -330,9 +330,12 @@ def tile_gaussianqueryassignment_t_kernel(
             gfbs[j] = gfb
 
         def t1(j):
-            tt = psum.tile([P, 8, P], BF16, tag="t1", bufs=2)
-            for a in range(8):
-                nc.tensor.transpose(tt[:, a, :], gfbs[j][:, P * a:P * a + P], ident_b[:])
+            words_j = gfbs[j][:].bitcast(F32)
+            tt = psum.tile([P, 2, 2, P], F32, tag="t1", bufs=2)
+            for h in range(2):
+                for u in range(2):
+                    c0 = P * (2 * h + u)
+                    nc.tensor.transpose(tt[:, h, u, :], words_j[:, c0:c0 + P], ident_f[:])
             t1s[j] = tt
 
         def t1_evac(j):
@@ -342,8 +345,8 @@ def tile_gaussianqueryassignment_t_kernel(
                 g2s[g] = grouped
             copy_out(
                 1,
-                g2s[g][:, :, P * b:P * b + P, :],
-                t1s[j][:].rearrange("p (g t) n -> p g n t", t=4),
+                g2s[g][:].bitcast(F32)[:, :, P * b:P * b + P, :],
+                t1s[j][:].rearrange("p h u n -> p h n u"),
             )
 
         def q2(g):

@@ -267,7 +267,7 @@ def tile_gaussianqueryassignment_t_kernel(
             if half == 0:
                 grouped = work.tile([P, widths[g] * G], BF16, align_bytes=64, tag="g0")
                 g0s[g] = grouped
-            word_copy(0, g0s[g], 2 * half, xts[g])
+            word_copy(1, g0s[g], 2 * half, xts[g])
 
         def q0(g):
             codes = work.tile([P, widths[g] * P], U32, align_bytes=64, tag="codes0", bufs=3)

@@ -225,7 +225,6 @@ def tile_gaussianqueryassignment_t_kernel(
         vs = {}
         sss = {}
         rns = {}
-        zeros = {}
         gfbs = {}
         t1s = {}
         g2s = {}
@@ -323,10 +322,7 @@ def tile_gaussianqueryassignment_t_kernel(
         def scale(j):
             g, b = blocks[j]
             gfb = work.tile([P, D], BF16, tag="gfb", bufs=4)
-            nc.gpsimd.tensor_scalar(
-                out=gfb[:], in0=vs[j][:], scalar1=rns[g][:, b:b + 1], scalar2=zeros[j][:, 0:1],
-                op0=ALU.mult, op1=ALU.add,
-            )
+            nc.vector.tensor_scalar_mul(out=gfb[:], in0=vs[j][:], scalar1=rns[g][:, b:b + 1])
             gfbs[j] = gfb
 
         def t1(j):
@@ -510,10 +506,6 @@ def tile_gaussianqueryassignment_t_kernel(
             g = at["q0"].get(tick)
             if g is not None:
                 q0(g)
-            if is_block(tick + 3):
-                zero = small.tile([P, 1], F32, tag="zero", bufs=3)
-                nc.vector.memset(zero[:], 0.0)
-                zeros[tick + 3] = zero
             if tick == -10:
                 pack_w("g", "u", 4)
             if tick == -7:

@@ -225,6 +225,7 @@ def tile_gaussianqueryassignment_t_kernel(
         vs = {}
         sss = {}
         rns = {}
+        zeros = {}
         gfbs = {}
         t1s = {}
         g2s = {}
@@ -322,7 +323,13 @@ def tile_gaussianqueryassignment_t_kernel(
         def scale(j):
             g, b = blocks[j]
             gfb = work.tile([P, D], BF16, tag="gfb", bufs=4)
-            nc.vector.tensor_scalar_mul(out=gfb[:], in0=vs[j][:], scalar1=rns[g][:, b:b + 1])
+            if b % 2 == 0:
+                nc.gpsimd.tensor_scalar(
+                    out=gfb[:], in0=vs[j][:], scalar1=rns[g][:, b:b + 1], scalar2=zeros[j][:, 0:1],
+                    op0=ALU.mult, op1=ALU.add,
+                )
+            else:
+                nc.vector.tensor_scalar_mul(out=gfb[:], in0=vs[j][:], scalar1=rns[g][:, b:b + 1])
             gfbs[j] = gfb
 
         def t1(j):
@@ -466,8 +473,8 @@ def tile_gaussianqueryassignment_t_kernel(
                 expo(g)
             if is_block(tick + 6):
                 square(tick + 6)
-            if is_block(tick + 2):
-                scale(tick + 2)
+            if is_block(tick + 1):
+                scale(tick + 1)
             g = at["rn"].get(tick)
             if g is not None:
                 inverse_norms(g)
@@ -506,6 +513,10 @@ def tile_gaussianqueryassignment_t_kernel(
             g = at["q0"].get(tick)
             if g is not None:
                 q0(g)
+            if is_block(tick + 2) and blocks[tick + 2][1] % 2 == 0:
+                zero = small.tile([P, 1], F32, tag="zero", bufs=3)
+                nc.vector.memset(zero[:], 0.0)
+                zeros[tick + 2] = zero
             if tick == -10:
                 pack_w("g", "u", 4)
             if tick == -7:

@@ -72,15 +72,15 @@ def tile_gaussianqueryassignment_t_kernel(
             e = last[g]
             at["t0a"][f - 15] = g
             at["eva"][f - 14] = g
-            at["q0"][f - 9] = g
+            at["q0"][f - 12 if g == 0 else f - 9] = g
             at["rn"][f - 3] = g
             at["q2"][e + 3] = g
             if g != QUERIES:
                 late = 2 if g < QUERIES else 0
                 at["load_x"][f - 26] = g
                 at["load_cen"][f - 8] = g
-                at["t0b"][f - 13] = g
-                at["evb"][f - 12] = g
+                at["t0b"][f - 14] = g
+                at["evb"][f - 13] = g
                 at["abs0"][f + 1] = g
                 at["abs1"][f + 2] = g
                 at["abs2"][f + 3] = g
@@ -95,25 +95,31 @@ def tile_gaussianqueryassignment_t_kernel(
         make_identity(nc, ident_b[:])
         neg_half = const.tile([P, 4], F32)
         nc.vector.memset(neg_half[:], -0.5)
+        ones = const.tile([P, 1], F32)
+        nc.vector.memset(ones[:], 1.0)
 
         misc = setup.tile([P, P], BF16)
         nc.vector.memset(misc[:], 0.0)
-        nc.scalar.dma_start(
-            out=misc[0:64, :], in_=keep_score[0].rearrange("t (b p) -> (t b) p", p=P)
-        )
-        nc.scalar.dma_start(out=misc[64:66, :], in_=presence_logit[0])
         pres_b = setup.tile([P, T * M], BF16)
-        nc.scalar.dma_start(
-            out=pres_b[:], in_=presence_logit[0].rearrange("t m -> (t m)").partition_broadcast(P)
-        )
         box = setup.tile([P, T, 7], BF16)
-        nc.scalar.dma_start(out=box[:], in_=query_box3d[0].rearrange("t m c -> m t c"))
         bgb = setup.tile([P, 1], BF16)
-        nc.scalar.dma_start(out=bgb[:], in_=background_bias.partition_broadcast(P))
         bg_b = const.tile([P, D], BF16)
-        nc.scalar.dma_start(out=bg_b[:], in_=bg.partition_broadcast(P))
         bq_b = const.tile([P, D], BF16)
-        nc.scalar.dma_start(out=bq_b[:], in_=bq.partition_broadcast(P))
+        warm = setup.tile([P, 1], F32)
+        nc.scalar.activation(out=warm[:], in_=neg_half[:, 0:1], func=ACT.Square)
+
+        def load_small():
+            nc.sync.dma_start(
+                out=misc[0:64, :], in_=keep_score[0].rearrange("t (b p) -> (t b) p", p=P)
+            )
+            nc.sync.dma_start(out=misc[64:66, :], in_=presence_logit[0])
+            nc.sync.dma_start(
+                out=pres_b[:], in_=presence_logit[0].rearrange("t m -> (t m)").partition_broadcast(P)
+            )
+            nc.sync.dma_start(out=box[:], in_=query_box3d[0].rearrange("t m c -> m t c"))
+            nc.sync.dma_start(out=bgb[:], in_=background_bias.partition_broadcast(P))
+            nc.sync.dma_start(out=bq_b[:], in_=bq.partition_broadcast(P))
+
         q_raw = setup.tile([P, T * G], BF16)
 
         def copy_out(which, out_ap, in_ap):
@@ -148,16 +154,15 @@ def tile_gaussianqueryassignment_t_kernel(
             w_codes[name] = const.tile([P, D], U32, align_bytes=64, name="w_codes_" + name)
             w_scales[name] = const.tile([P, D], U8, align_bytes=64, name="w_scales_" + name)
 
-        def pack_w(name, tag, bufs):
-            for h in range(2):
-                grouped_w = setup.tile([P, 4 * G], BF16, align_bytes=64, tag="g0w", bufs=2)
-                for i in range(2):
-                    xt = word_transposes(w_raws[name][:].bitcast(F32), 4 * h + 2 * i, tag, bufs)
-                    word_copy(i, grouped_w, 2 * i, xt)
-                dcols = slice(512 * h, 512 * h + 512)
-                nc.vector.quantize_mx(
-                    out=w_codes[name][:, dcols].bitcast(FP8X4), scales=w_scales[name][:, dcols], in_=grouped_w[:]
-                )
+        def pack_w(name, h, tag, bufs):
+            grouped_w = setup.tile([P, 4 * G], BF16, align_bytes=64, tag="g0w", bufs=2)
+            for i in range(2):
+                xt = word_transposes(w_raws[name][:].bitcast(F32), 4 * h + 2 * i, tag, bufs)
+                word_copy(i, grouped_w, 2 * i, xt)
+            dcols = slice(512 * h, 512 * h + 512)
+            nc.vector.quantize_mx(
+                out=w_codes[name][:, dcols].bitcast(FP8X4), scales=w_scales[name][:, dcols], in_=grouped_w[:]
+            )
 
         q_codes = const.tile([P, 2 * T * M], U32, align_bytes=64)
         q_scales = const.tile([P, 2 * T * M], U8, align_bytes=64)
@@ -184,7 +189,7 @@ def tile_gaussianqueryassignment_t_kernel(
             nc.vector.tensor_reduce(
                 out=pmax[:], in_=pres_b[:].rearrange("p (t m) -> p t m", m=M), axis=AX.X, op=ALU.max
             )
-            misc_t = psum.tile([P, P], BF16, tag="t0")
+            misc_t = psum.tile([P, P], BF16, tag="ep")
             nc.tensor.transpose(misc_t[:], misc[:], ident_b[:])
             nc.vector.scalar_tensor_tensor(
                 out=bias_p[:], in0=misc_t[:, 64:66], scalar=-6.0, in1=pmax[:], op0=ALU.add, op1=ALU.subtract
@@ -232,11 +237,15 @@ def tile_gaussianqueryassignment_t_kernel(
         codes2 = {QUERIES: q_codes}
         scales2 = {QUERIES: q_scales}
         dists = {}
+        m1s = {}
         m2s = {}
+        tots = {}
+        rts = {}
         sims = {}
         ys = {}
         es = {}
         ets = {}
+        esums = {}
 
         def load_x(g):
             t = frame_of(g)
@@ -261,13 +270,13 @@ def tile_gaussianqueryassignment_t_kernel(
             cens[g] = cen
 
         def t0(g, half):
-            xts[g] = word_transposes(words[g], 2 * half, "t0", 1)
+            xts[g, half] = word_transposes(words[g], 2 * half, "tt", 3)
 
         def t0_evac(g, half):
             if half == 0:
                 grouped = work.tile([P, widths[g] * G], BF16, align_bytes=64, tag="g0")
                 g0s[g] = grouped
-            word_copy(1, g0s[g], 2 * half, xts[g])
+            word_copy(1, g0s[g], 2 * half, xts[g, half])
 
         def q0(g):
             codes = work.tile([P, widths[g] * P], U32, align_bytes=64, tag="codes0", bufs=3)
@@ -295,14 +304,14 @@ def tile_gaussianqueryassignment_t_kernel(
                 )
                 us[j].append(u)
 
-        def add_bias(j):
+        def add_bias(j, h):
             g, b = blocks[j]
             bias_b = bq_b if g == QUERIES else bg_b
-            v = vpool.tile([P, D], F32, tag="v")
-            for h in range(2):
-                dcols = slice(512 * h, 512 * h + 512)
-                nc.vector.tensor_tensor(out=v[:, dcols], in0=us[j][h][:], in1=bias_b[:, dcols], op=ALU.add)
-            vs[j] = v
+            if h == 0:
+                v = vpool.tile([P, D], F32, tag="v")
+                vs[j] = v
+            dcols = slice(512 * h, 512 * h + 512)
+            nc.vector.tensor_tensor(out=vs[j][:, dcols], in0=us[j][h][:], in1=bias_b[:, dcols], op=ALU.add)
 
         def square(j):
             g, b = blocks[j]
@@ -334,7 +343,7 @@ def tile_gaussianqueryassignment_t_kernel(
 
         def t1(j):
             words_j = gfbs[j][:].bitcast(F32)
-            tt = psum.tile([P, 2, 2, P], F32, tag="t1", bufs=2)
+            tt = psum.tile([P, 2, 2, P], F32, tag="tt", bufs=3)
             for h in range(2):
                 for u in range(2):
                     c0 = P * (2 * h + u)
@@ -375,12 +384,15 @@ def tile_gaussianqueryassignment_t_kernel(
                 scale=a6[:, t, c:c + 1], bias=nqa6[:, t, c:c + 1],
             )
 
-        def gate_max(g):
+        def gate_max_a(g):
             dist = dists[g]
             m1 = epool.tile([P, SB], F32, tag="m1")
             nc.vector.tensor_tensor(out=m1[:], in0=dist[:, 0, :], in1=dist[:, 1, :], op=ALU.max)
+            m1s[g] = m1
+
+        def gate_max_b(g):
             m2 = epool.tile([P, SB], F32, tag="m2", bufs=3)
-            nc.vector.tensor_tensor(out=m2[:], in0=m1[:], in1=dist[:, 2, :], op=ALU.max)
+            nc.vector.tensor_tensor(out=m2[:], in0=m1s[g][:], in1=dists[g][:, 2, :], op=ALU.max)
             m2s[g] = m2
 
         def s2(g):
@@ -413,25 +425,38 @@ def tile_gaussianqueryassignment_t_kernel(
             es[g] = e
 
         def t2(g):
+            sums = psum.tile([P, 4], F32, tag="tt", bufs=3)
+            for j in range(4):
+                nc.tensor.matmul(
+                    sums[:, j:j + 1], lhsT=es[g][:, P * j:P * j + P], rhs=ones[:], start=True, stop=True
+                )
+            esums[g] = sums
             e_t = psum.tile([P, 4, P], F32, tag="ep")
             for j in range(4):
                 nc.tensor.transpose(e_t[:, j, :], es[g][:, P * j:P * j + P], ident_f[:])
             ets[g] = e_t
 
+        def total(g):
+            tot = small.tile([P, 4], F32, tag="tot")
+            bc = slice(4 * sb_of(g), 4 * sb_of(g) + 4)
+            nc.vector.tensor_tensor(out=tot[:], in0=esums[g][:], in1=ebg[:, bc], op=ALU.add)
+            tots[g] = tot
+
+        def inverse_total(g):
+            rt = small.tile([P, 4], F32, tag="rt")
+            nc.vector.reciprocal(out=rt[:], in_=tots[g][:])
+            rts[g] = rt
+
         def finish(g):
             s = sb_of(g)
             e_t = ets[g]
+            rt = rts[g]
             bc = slice(4 * s, 4 * s + 4)
-            tot = small.tile([P, 4], F32, tag="tot")
-            nc.vector.tensor_reduce(out=tot[:], in_=e_t[:], axis=AX.X, op=ALU.add)
-            nc.vector.tensor_tensor(out=tot[:], in0=tot[:], in1=ebg[:, bc], op=ALU.add)
-            rt = small.tile([P, 4], F32, tag="rt")
-            nc.vector.reciprocal(out=rt[:], in_=tot[:])
             o = opool.tile([P, 4, M + 1], F32, tag="o")
-            nc.vector.tensor_tensor(out=o[:, :, 0], in0=rt[:], in1=ebg[:, bc], op=ALU.mult)
             nc.vector.tensor_tensor(
                 out=o[:, :, 1:M + 1], in0=e_t[:], in1=rt[:].unsqueeze(2).to_broadcast([P, 4, M]), op=ALU.mult
             )
+            nc.vector.tensor_tensor(out=o[:, :, 0], in0=rt[:], in1=ebg[:, bc], op=ALU.mult)
             nc.sync.dma_start(
                 out=out[0, SB * s:SB * s + SB, :].rearrange("(j p) c -> p j c", p=P), in_=o[:]
             )
@@ -445,29 +470,42 @@ def tile_gaussianqueryassignment_t_kernel(
                 load_x(g)
             if tick == -26:
                 load_w("g", Wg)
+                nc.sync.dma_start(out=bg_b[:], in_=bg.partition_broadcast(P))
                 nc.sync.dma_start(
                     out=q_raw[:].rearrange("p (t k) -> p t k", k=G), in_=query_feat[0].rearrange("t m k -> m t k")
                 )
                 load_w("q", Wq)
+                load_small()
             g = at["load_cen"].get(tick)
             if g is not None:
                 load_cen(g)
-            if tick == -16:
+            if tick == -10:
                 constants_a()
             if tick == -9:
                 constants_ln()
             if tick == -3:
                 constants_b()
-            g = at["t2"].get(tick)
-            if g is not None:
-                t2(g)
             if is_block(tick + 8):
                 s1(tick + 8)
             g = at["s2"].get(tick)
             if g is not None:
                 s2(g)
             if is_block(tick + 7):
-                add_bias(tick + 7)
+                add_bias(tick + 7, 0)
+            g = at["t2"].get(tick)
+            if g is not None:
+                total(g)
+            g = at["gmax"].get(tick)
+            if g is not None:
+                gate_max_a(g)
+            if is_block(tick + 7):
+                add_bias(tick + 7, 1)
+            g = at["t2"].get(tick)
+            if g is not None:
+                inverse_total(g)
+            g = at["gmax"].get(tick)
+            if g is not None:
+                gate_max_b(g)
             g = at["exp"].get(tick)
             if g is not None:
                 expo(g)
@@ -486,18 +524,21 @@ def tile_gaussianqueryassignment_t_kernel(
             g = at["t0b"].get(tick)
             if g is not None:
                 t0(g, 1)
+            g = at["exp"].get(tick)
+            if g is not None:
+                t2(g)
             if is_block(tick - 1):
                 t1_evac(tick - 1)
-            for c in range(3):
-                g = at["abs%d" % c].get(tick)
-                if g is not None:
-                    gate_abs(g, c)
             g = at["eva"].get(tick)
             if g is not None:
                 t0_evac(g, 0)
             g = at["evb"].get(tick)
             if g is not None:
                 t0_evac(g, 1)
+            for c in range(3):
+                g = at["abs%d" % c].get(tick)
+                if g is not None:
+                    gate_abs(g, c)
             g = at["s2"].get(tick)
             if g is not None:
                 logits(g)
@@ -507,9 +548,6 @@ def tile_gaussianqueryassignment_t_kernel(
             g = at["q2"].get(tick)
             if g is not None:
                 q2(g)
-            g = at["gmax"].get(tick)
-            if g is not None:
-                gate_max(g)
             g = at["q0"].get(tick)
             if g is not None:
                 q0(g)
@@ -517,7 +555,10 @@ def tile_gaussianqueryassignment_t_kernel(
                 zero = small.tile([P, 1], F32, tag="zero", bufs=3)
                 nc.vector.memset(zero[:], 0.0)
                 zeros[tick + 2] = zero
-            if tick == -10:
-                pack_w("g", "u", 4)
+            if tick == -14:
+                pack_w("g", 0, "u", 4)
+            if tick == -13:
+                pack_w("g", 1, "u", 4)
             if tick == -7:
-                pack_w("q", "t1", 2)
+                pack_w("q", 0, "tt", 3)
+                pack_w("q", 1, "tt", 3)

@@ -239,7 +239,6 @@ def tile_gaussianqueryassignment_t_kernel(
         dists = {}
         m1s = {}
         m2s = {}
-        tots = {}
         rts = {}
         sims = {}
         ys = {}
@@ -332,13 +331,15 @@ def tile_gaussianqueryassignment_t_kernel(
         def scale(j):
             g, b = blocks[j]
             gfb = work.tile([P, D], BF16, tag="gfb", bufs=4)
-            if b % 2 == 0:
-                nc.gpsimd.tensor_scalar(
-                    out=gfb[:], in0=vs[j][:], scalar1=rns[g][:, b:b + 1], scalar2=zeros[j][:, 0:1],
-                    op0=ALU.mult, op1=ALU.add,
+            share = D if b % 2 == 0 else D // 2
+            nc.gpsimd.tensor_scalar(
+                out=gfb[:, 0:share], in0=vs[j][:, 0:share], scalar1=rns[g][:, b:b + 1],
+                scalar2=zeros[j][:, 0:1], op0=ALU.mult, op1=ALU.add,
+            )
+            if share < D:
+                nc.vector.tensor_scalar_mul(
+                    out=gfb[:, share:D], in0=vs[j][:, share:D], scalar1=rns[g][:, b:b + 1]
                 )
-            else:
-                nc.vector.tensor_scalar_mul(out=gfb[:], in0=vs[j][:], scalar1=rns[g][:, b:b + 1])
             gfbs[j] = gfb
 
         def t1(j):
@@ -425,10 +426,14 @@ def tile_gaussianqueryassignment_t_kernel(
             es[g] = e
 
         def t2(g):
-            sums = psum.tile([P, 4], F32, tag="tt", bufs=3)
+            bc = slice(4 * sb_of(g), 4 * sb_of(g) + 4)
+            sums = psum.tile([P, 2, 4], F32, tag="tt", bufs=3)
+            nc.tensor.matmul(
+                sums[:], lhsT=ident_f[:], rhs=ebg[:, bc].unsqueeze(1).to_broadcast([P, 2, 4]), start=True, stop=False
+            )
             for j in range(4):
                 nc.tensor.matmul(
-                    sums[:, j:j + 1], lhsT=es[g][:, P * j:P * j + P], rhs=ones[:], start=True, stop=True
+                    sums[:, 0, j:j + 1], lhsT=es[g][:, P * j:P * j + P], rhs=ones[:], start=False, stop=(j == 3)
                 )
             esums[g] = sums
             e_t = psum.tile([P, 4, P], F32, tag="ep")
@@ -436,27 +441,20 @@ def tile_gaussianqueryassignment_t_kernel(
                 nc.tensor.transpose(e_t[:, j, :], es[g][:, P * j:P * j + P], ident_f[:])
             ets[g] = e_t
 
-        def total(g):
-            tot = small.tile([P, 4], F32, tag="tot")
-            bc = slice(4 * sb_of(g), 4 * sb_of(g) + 4)
-            nc.vector.tensor_tensor(out=tot[:], in0=esums[g][:], in1=ebg[:, bc], op=ALU.add)
-            tots[g] = tot
-
         def inverse_total(g):
             rt = small.tile([P, 4], F32, tag="rt")
-            nc.vector.reciprocal(out=rt[:], in_=tots[g][:])
+            nc.vector.reciprocal(out=rt[:], in_=esums[g][:, 0, :])
             rts[g] = rt
 
         def finish(g):
             s = sb_of(g)
             e_t = ets[g]
             rt = rts[g]
-            bc = slice(4 * s, 4 * s + 4)
             o = opool.tile([P, 4, M + 1], F32, tag="o")
             nc.vector.tensor_tensor(
                 out=o[:, :, 1:M + 1], in0=e_t[:], in1=rt[:].unsqueeze(2).to_broadcast([P, 4, M]), op=ALU.mult
             )
-            nc.vector.tensor_tensor(out=o[:, :, 0], in0=rt[:], in1=ebg[:, bc], op=ALU.mult)
+            nc.vector.tensor_tensor(out=o[:, :, 0], in0=esums[g][:, 1, :], in1=rt[:], op=ALU.mult)
             nc.sync.dma_start(
                 out=out[0, SB * s:SB * s + SB, :].rearrange("(j p) c -> p j c", p=P), in_=o[:]
             )
@@ -494,18 +492,12 @@ def tile_gaussianqueryassignment_t_kernel(
                 add_bias(tick + 7, 0)
             g = at["t2"].get(tick)
             if g is not None:
-                total(g)
+                inverse_total(g)
+            if is_block(tick + 7):
+                add_bias(tick + 7, 1)
             g = at["gmax"].get(tick)
             if g is not None:
                 gate_max_a(g)
-            if is_block(tick + 7):
-                add_bias(tick + 7, 1)
-            g = at["t2"].get(tick)
-            if g is not None:
-                inverse_total(g)
-            g = at["gmax"].get(tick)
-            if g is not None:
-                gate_max_b(g)
             g = at["exp"].get(tick)
             if g is not None:
                 expo(g)
@@ -513,6 +505,9 @@ def tile_gaussianqueryassignment_t_kernel(
                 square(tick + 6)
             if is_block(tick + 1):
                 scale(tick + 1)
+            g = at["gmax"].get(tick)
+            if g is not None:
+                gate_max_b(g)
             g = at["rn"].get(tick)
             if g is not None:
                 inverse_norms(g)
@@ -551,7 +546,7 @@ def tile_gaussianqueryassignment_t_kernel(
             g = at["q0"].get(tick)
             if g is not None:
                 q0(g)
-            if is_block(tick + 2) and blocks[tick + 2][1] % 2 == 0:
+            if is_block(tick + 2):
                 zero = small.tile([P, 1], F32, tag="zero", bufs=3)
                 nc.vector.memset(zero[:], 0.0)
                 zeros[tick + 2] = zero

@@ -63,6 +63,9 @@ def tile_gaussianqueryassignment_t_kernel(
         def n0_of(g):
             return SB * (sb_of(g) % (NSB // T))
 
+        def gpsimd_columns(j):
+            return (D, D // 2, D, 0)[blocks[j][1]]
+
         at = {}
         for kind in ("load_x", "load_cen", "t0a", "eva", "t0b", "evb", "q0", "rn", "abs0", "abs1", "abs2",
                      "gmax", "q2", "s2", "exp", "t2"):
@@ -70,17 +73,18 @@ def tile_gaussianqueryassignment_t_kernel(
         for g, nb in enumerate(widths):
             f = first[g]
             e = last[g]
-            at["t0a"][f - 15] = g
-            at["eva"][f - 14] = g
-            at["q0"][f - 12 if g == 0 else f - 9] = g
+            lead = 4 if g == 0 else 0
+            at["t0a"][f - 12 - lead] = g
+            at["eva"][f - 11 - lead] = g
+            at["q0"][f - 9 - lead] = g
             at["rn"][f - 3] = g
             at["q2"][e + 3] = g
             if g != QUERIES:
                 late = 2 if g < QUERIES else 0
                 at["load_x"][f - 26] = g
                 at["load_cen"][f - 8] = g
-                at["t0b"][f - 14] = g
-                at["evb"][f - 13] = g
+                at["t0b"][f - 11 - lead] = g
+                at["evb"][f - 10 - lead] = g
                 at["abs0"][f + 1] = g
                 at["abs1"][f + 2] = g
                 at["abs2"][f + 3] = g
@@ -154,14 +158,20 @@ def tile_gaussianqueryassignment_t_kernel(
             w_codes[name] = const.tile([P, D], U32, align_bytes=64, name="w_codes_" + name)
             w_scales[name] = const.tile([P, D], U8, align_bytes=64, name="w_scales_" + name)
 
-        def pack_w(name, h, tag, bufs):
-            grouped_w = setup.tile([P, 4 * G], BF16, align_bytes=64, tag="g0w", bufs=2)
-            for i in range(2):
-                xt = word_transposes(w_raws[name][:].bitcast(F32), 4 * h + 2 * i, tag, bufs)
-                word_copy(i, grouped_w, 2 * i, xt)
+        grouped_ws = {}
+
+        def regroup_w(name, h, i, tag, bufs):
+            if i == 0:
+                grouped_w = setup.tile([P, 4 * G], BF16, align_bytes=64, tag="g0w", bufs=2)
+                grouped_ws[name, h] = grouped_w
+            xt = word_transposes(w_raws[name][:].bitcast(F32), 4 * h + 2 * i, tag, bufs)
+            word_copy(i, grouped_ws[name, h], 2 * i, xt)
+
+        def quantize_w(name, h):
             dcols = slice(512 * h, 512 * h + 512)
             nc.vector.quantize_mx(
-                out=w_codes[name][:, dcols].bitcast(FP8X4), scales=w_scales[name][:, dcols], in_=grouped_w[:]
+                out=w_codes[name][:, dcols].bitcast(FP8X4), scales=w_scales[name][:, dcols],
+                in_=grouped_ws[name, h][:],
             )
 
         q_codes = const.tile([P, 2 * T * M], U32, align_bytes=64)
@@ -176,49 +186,99 @@ def tile_gaussianqueryassignment_t_kernel(
         l1 = setup.tile([P, 64], F32)
         l2 = setup.tile([P, 64], F32)
 
-        def constants_a():
+        misc_ts = []
+        sizes = []
+
+        def transpose_misc():
+            misc_t = psum.tile([P, P], BF16, tag="ep")
+            nc.tensor.transpose(misc_t[:], misc[:], ident_b[:])
+            misc_ts.append(misc_t)
+
+        def box_sizes():
             size = setup.tile([P, T, 3], F32)
             nc.vector.scalar_tensor_tensor(
                 out=size[:], in0=box[:, :, 3:6], scalar=-1.0, in1=box[:, :, 3:6], op0=ALU.mult, op1=ALU.max
             )
-            nc.vector.tensor_scalar(out=size[:], in0=size[:], scalar1=0.5, scalar2=1.5, op0=ALU.max, op1=ALU.mult)
-            nc.vector.reciprocal(out=a6[:], in_=size[:])
+            sizes.append(size)
+
+        def box_floor():
+            nc.vector.tensor_scalar(
+                out=sizes[0][:], in0=sizes[0][:], scalar1=0.5, scalar2=1.5, op0=ALU.max, op1=ALU.mult
+            )
+
+        def box_inverse():
+            nc.vector.reciprocal(out=a6[:], in_=sizes[0][:])
+
+        def box_shift():
             nc.vector.scalar_tensor_tensor(
                 out=nqa6[:], in0=box[:, :, 0:3], scalar=-1.0, in1=a6[:], op0=ALU.mult, op1=ALU.mult
             )
+
+        def presence_max():
             nc.vector.tensor_reduce(
                 out=pmax[:], in_=pres_b[:].rearrange("p (t m) -> p t m", m=M), axis=AX.X, op=ALU.max
             )
-            misc_t = psum.tile([P, P], BF16, tag="ep")
-            nc.tensor.transpose(misc_t[:], misc[:], ident_b[:])
-            nc.vector.scalar_tensor_tensor(
-                out=bias_p[:], in0=misc_t[:, 64:66], scalar=-6.0, in1=pmax[:], op0=ALU.add, op1=ALU.subtract
-            )
-            nc.vector.tensor_scalar(
-                out=ks[:], in0=misc_t[:, 0:64], scalar1=1e-4, scalar2=1.0 - 1e-4, op0=ALU.max, op1=ALU.min
-            )
 
-        def constants_ln():
+        def keep_clip():
+            nc.vector.tensor_scalar(
+                out=ks[:], in0=misc_ts[0][:, 0:64], scalar1=1e-4, scalar2=1.0 - 1e-4, op0=ALU.max, op1=ALU.min
+            )
             nc.scalar.activation(out=l1[:], in_=ks[:], func=ACT.Ln)
             nc.scalar.activation(out=l2[:], in_=ks[:], func=ACT.Ln, scale=-1.0, bias=1.0)
 
-        def constants_b():
-            dl = setup.tile([P, 64], F32)
-            nc.vector.tensor_tensor(out=dl[:], in0=l1[:], in1=l2[:], op=ALU.subtract)
-            bgb9 = setup.tile([P, 1], F32)
+        def query_bias():
+            nc.vector.scalar_tensor_tensor(
+                out=bias_p[:], in0=misc_ts[0][:, 64:66], scalar=-6.0, in1=pmax[:], op0=ALU.add, op1=ALU.subtract
+            )
+
+        dl = setup.tile([P, 64], F32)
+        bgb9 = setup.tile([P, 1], F32)
+        cb = setup.tile([P, T], F32)
+        lb = setup.tile([P, 64], F32)
+
+        def background_shift():
             nc.vector.tensor_scalar_add(out=bgb9[:], in0=bgb[:], scalar1=-9.0)
-            cb = setup.tile([P, T], F32)
+
+        def background_bias_of_frames():
             nc.vector.tensor_scalar(
                 out=cb[:], in0=pmax[:], scalar1=-1.0, scalar2=bgb9[:, 0:1], op0=ALU.mult, op1=ALU.add
             )
-            lb = setup.tile([P, 64], F32)
+
+        def log_odds():
+            nc.vector.tensor_tensor(out=dl[:], in0=l1[:], in1=l2[:], op=ALU.subtract)
+
+        def background_logits():
             for t in range(T):
                 nc.vector.tensor_scalar(
                     out=lb[:, 32 * t:32 * t + 32], in0=dl[:, 32 * t:32 * t + 32],
                     scalar1=-0.5, scalar2=cb[:, t:t + 1], op0=ALU.mult, op1=ALU.add,
                 )
+
+        def background_exp():
             nc.vector.tensor_scalar_min(out=lb[:], in0=lb[:], scalar1=80.0)
             nc.scalar.activation(out=ebg[:], in_=lb[:], func=ACT.Exp)
+
+        chores = [
+            lambda: regroup_w("q", 0, 0, "tt", 3),
+            lambda: regroup_w("q", 0, 1, "tt", 3),
+            lambda: quantize_w("q", 0),
+            lambda: regroup_w("q", 1, 0, "tt", 3),
+            lambda: regroup_w("q", 1, 1, "tt", 3),
+            lambda: quantize_w("q", 1),
+            transpose_misc,
+            box_sizes,
+            box_floor,
+            box_inverse,
+            box_shift,
+            presence_max,
+            keep_clip,
+            query_bias,
+            background_shift,
+            background_bias_of_frames,
+            log_odds,
+            background_logits,
+            background_exp,
+        ]
 
         words = {QUERIES: q_raw[:].bitcast(F32)}
         cens = {}
@@ -311,6 +371,8 @@ def tile_gaussianqueryassignment_t_kernel(
                 vs[j] = v
             dcols = slice(512 * h, 512 * h + 512)
             nc.vector.tensor_tensor(out=vs[j][:, dcols], in0=us[j][h][:], in1=bias_b[:, dcols], op=ALU.add)
+            if chores:
+                chores.pop(0)()
 
         def square(j):
             g, b = blocks[j]
@@ -331,11 +393,12 @@ def tile_gaussianqueryassignment_t_kernel(
         def scale(j):
             g, b = blocks[j]
             gfb = work.tile([P, D], BF16, tag="gfb", bufs=4)
-            share = D if b % 2 == 0 else D // 2
-            nc.gpsimd.tensor_scalar(
-                out=gfb[:, 0:share], in0=vs[j][:, 0:share], scalar1=rns[g][:, b:b + 1],
-                scalar2=zeros[j][:, 0:1], op0=ALU.mult, op1=ALU.add,
-            )
+            share = gpsimd_columns(j)
+            if share > 0:
+                nc.gpsimd.tensor_scalar(
+                    out=gfb[:, 0:share], in0=vs[j][:, 0:share], scalar1=rns[g][:, b:b + 1],
+                    scalar2=zeros[j][:, 0:1], op0=ALU.mult, op1=ALU.add,
+                )
             if share < D:
                 nc.vector.tensor_scalar_mul(
                     out=gfb[:, share:D], in0=vs[j][:, share:D], scalar1=rns[g][:, b:b + 1]
@@ -477,12 +540,6 @@ def tile_gaussianqueryassignment_t_kernel(
             g = at["load_cen"].get(tick)
             if g is not None:
                 load_cen(g)
-            if tick == -10:
-                constants_a()
-            if tick == -9:
-                constants_ln()
-            if tick == -3:
-                constants_b()
             if is_block(tick + 8):
                 s1(tick + 8)
             g = at["s2"].get(tick)
@@ -546,14 +603,12 @@ def tile_gaussianqueryassignment_t_kernel(
             g = at["q0"].get(tick)
             if g is not None:
                 q0(g)
-            if is_block(tick + 2):
+            if is_block(tick + 2) and gpsimd_columns(tick + 2) > 0:
                 zero = small.tile([P, 1], F32, tag="zero", bufs=3)
                 nc.vector.memset(zero[:], 0.0)
                 zeros[tick + 2] = zero
-            if tick == -14:
-                pack_w("g", 0, "u", 4)
-            if tick == -13:
-                pack_w("g", 1, "u", 4)
-            if tick == -7:
-                pack_w("q", 0, "tt", 3)
-                pack_w("q", 1, "tt", 3)
+            if -14 <= tick <= -13:
+                h = tick + 14
+                regroup_w("g", h, 0, "u", 4)
+                regroup_w("g", h, 1, "u", 4)
+                quantize_w("g", h)

@@ -73,18 +73,18 @@ def tile_gaussianqueryassignment_t_kernel(
         for g, nb in enumerate(widths):
             f = first[g]
             e = last[g]
-            lead = 4 if g == 0 else 0
-            at["t0a"][f - 12 - lead] = g
-            at["eva"][f - 11 - lead] = g
-            at["q0"][f - 9 - lead] = g
+            lead = (16, 11, 12)[g] if g < 3 else 15
+            at["t0a"][f - lead] = g
+            at["eva"][f - lead + 1] = g
+            at["q0"][f - (13 if g == 0 else 9)] = g
             at["rn"][f - 3] = g
             at["q2"][e + 3] = g
             if g != QUERIES:
                 late = 2 if g < QUERIES else 0
                 at["load_x"][f - 26] = g
                 at["load_cen"][f - 8] = g
-                at["t0b"][f - 11 - lead] = g
-                at["evb"][f - 10 - lead] = g
+                at["t0b"][f - lead + 1] = g
+                at["evb"][f - lead + 2] = g
                 at["abs0"][f + 1] = g
                 at["abs1"][f + 2] = g
                 at["abs2"][f + 3] = g

@@ -53,6 +53,7 @@ def tile_gaussianqueryassignment_t_kernel(
                 blocks.append((g, b))
             last.append(len(blocks) - 1)
         nblocks = len(blocks)
+        final = len(widths) - 1
 
         def sb_of(g):
             return g if g < QUERIES else g - 1
@@ -64,7 +65,12 @@ def tile_gaussianqueryassignment_t_kernel(
             return SB * (sb_of(g) % (NSB // T))
 
         def gpsimd_columns(j):
-            return (D, D // 2, D, 0)[blocks[j][1]]
+            g, b = blocks[j]
+            return 0 if g == final else (D, D // 2, D, 0)[b]
+
+        turns = {}
+        for j, (g, b) in enumerate(blocks):
+            turns.setdefault(j if g < final else first[g] + b // 2, []).append(j)
 
         at = {}
         for kind in ("load_x", "load_cen", "t0a", "eva", "t0b", "evb", "q0", "rn", "abs0", "abs1", "abs2",
@@ -72,7 +78,7 @@ def tile_gaussianqueryassignment_t_kernel(
             at[kind] = {}
         for g, nb in enumerate(widths):
             f = first[g]
-            e = last[g]
+            e = last[g] if g < final else max(turns) - 1
             lead = (16, 11, 12)[g] if g < 3 else 15
             at["t0a"][f - lead] = g
             at["eva"][f - lead + 1] = g
@@ -82,13 +88,13 @@ def tile_gaussianqueryassignment_t_kernel(
             if g != QUERIES:
                 late = 2 if g < QUERIES else 0
                 at["load_x"][f - 26] = g
-                at["load_cen"][f - 8] = g
+                if g > 0:
+                    at["load_cen"][f - 8] = g
                 at["t0b"][f - lead + 1] = g
                 at["evb"][f - lead + 2] = g
-                at["abs0"][f + 1] = g
-                at["abs1"][f + 2] = g
-                at["abs2"][f + 3] = g
-                at["gmax"][f + 4] = g
+                gate = (f + 1, f + 2, f + 3, f + 4) if g > 0 else (-8, -8, -8, -6)
+                for kind, tick in zip(("abs0", "abs1", "abs2", "gmax"), gate):
+                    at[kind][tick] = g
                 at["s2"][e + 4 + late] = g
                 at["exp"][e + 5 + late] = g
                 at["t2"][e + 6 + late] = g
@@ -110,17 +116,18 @@ def tile_gaussianqueryassignment_t_kernel(
         bg_b = const.tile([P, D], BF16)
         bq_b = const.tile([P, D], BF16)
         warm = setup.tile([P, 1], F32)
-        nc.scalar.activation(out=warm[:], in_=neg_half[:, 0:1], func=ACT.Square)
+        nc.scalar.activation(out=warm[:], in_=ones[:], func=ACT.Ln)
 
-        def load_small():
+        def load_keep():
             nc.sync.dma_start(
                 out=misc[0:64, :], in_=keep_score[0].rearrange("t (b p) -> (t b) p", p=P)
             )
             nc.sync.dma_start(out=misc[64:66, :], in_=presence_logit[0])
+
+        def load_small():
             nc.sync.dma_start(
                 out=pres_b[:], in_=presence_logit[0].rearrange("t m -> (t m)").partition_broadcast(P)
             )
-            nc.sync.dma_start(out=box[:], in_=query_box3d[0].rearrange("t m c -> m t c"))
             nc.sync.dma_start(out=bgb[:], in_=background_bias.partition_broadcast(P))
             nc.sync.dma_start(out=bq_b[:], in_=bq.partition_broadcast(P))
 
@@ -265,13 +272,7 @@ def tile_gaussianqueryassignment_t_kernel(
             lambda: regroup_w("q", 1, 0, "tt", 3),
             lambda: regroup_w("q", 1, 1, "tt", 3),
             lambda: quantize_w("q", 1),
-            transpose_misc,
-            box_sizes,
-            box_floor,
-            box_inverse,
-            box_shift,
             presence_max,
-            keep_clip,
             query_bias,
             background_shift,
             background_bias_of_frames,
@@ -335,7 +336,7 @@ def tile_gaussianqueryassignment_t_kernel(
             if half == 0:
                 grouped = work.tile([P, widths[g] * G], BF16, align_bytes=64, tag="g0")
                 g0s[g] = grouped
-            word_copy(1, g0s[g], 2 * half, xts[g, half])
+            word_copy(0 if half == 1 and g % 2 == 0 else 1, g0s[g], 2 * half, xts[g, half])
 
         def q0(g):
             codes = work.tile([P, widths[g] * P], U32, align_bytes=64, tag="codes0", bufs=3)
@@ -371,8 +372,6 @@ def tile_gaussianqueryassignment_t_kernel(
                 vs[j] = v
             dcols = slice(512 * h, 512 * h + 512)
             nc.vector.tensor_tensor(out=vs[j][:, dcols], in0=us[j][h][:], in1=bias_b[:, dcols], op=ALU.add)
-            if chores:
-                chores.pop(0)()
 
         def square(j):
             g, b = blocks[j]
@@ -455,7 +454,7 @@ def tile_gaussianqueryassignment_t_kernel(
             m1s[g] = m1
 
         def gate_max_b(g):
-            m2 = epool.tile([P, SB], F32, tag="m2", bufs=3)
+            m2 = epool.tile([P, SB], F32, tag="m2", bufs=4)
             nc.vector.tensor_tensor(out=m2[:], in0=m1s[g][:], in1=dists[g][:, 2, :], op=ALU.max)
             m2s[g] = m2
 
@@ -530,8 +529,11 @@ def tile_gaussianqueryassignment_t_kernel(
             if g is not None:
                 load_x(g)
             if tick == -26:
+                load_keep()
                 load_w("g", Wg)
+                nc.sync.dma_start(out=box[:], in_=query_box3d[0].rearrange("t m c -> m t c"))
                 nc.sync.dma_start(out=bg_b[:], in_=bg.partition_broadcast(P))
+                load_cen(0)
                 nc.sync.dma_start(
                     out=q_raw[:].rearrange("p (t k) -> p t k", k=G), in_=query_feat[0].rearrange("t m k -> m t k")
                 )
@@ -560,16 +562,22 @@ def tile_gaussianqueryassignment_t_kernel(
                 expo(g)
             if is_block(tick + 6):
                 square(tick + 6)
-            if is_block(tick + 1):
-                scale(tick + 1)
+            g = at["q2"].get(tick)
+            if g is not None:
+                q2(g)
+            for j in turns.get(tick + 1, []):
+                scale(j)
             g = at["gmax"].get(tick)
             if g is not None:
                 gate_max_b(g)
             g = at["rn"].get(tick)
             if g is not None:
                 inverse_norms(g)
-            if is_block(tick):
-                t1(tick)
+            for step in chores[0:2] if tick >= -7 else []:
+                step()
+                chores.remove(step)
+            for j in turns.get(tick, []):
+                t1(j)
             g = at["t0a"].get(tick)
             if g is not None:
                 t0(g, 0)
@@ -579,8 +587,8 @@ def tile_gaussianqueryassignment_t_kernel(
             g = at["exp"].get(tick)
             if g is not None:
                 t2(g)
-            if is_block(tick - 1):
-                t1_evac(tick - 1)
+            for j in turns.get(tick - 1, []):
+                t1_evac(j)
             g = at["eva"].get(tick)
             if g is not None:
                 t0_evac(g, 0)
@@ -597,9 +605,6 @@ def tile_gaussianqueryassignment_t_kernel(
             g = at["t2"].get(tick)
             if g is not None:
                 finish(g)
-            g = at["q2"].get(tick)
-            if g is not None:
-                q2(g)
             g = at["q0"].get(tick)
             if g is not None:
                 q0(g)
@@ -607,8 +612,17 @@ def tile_gaussianqueryassignment_t_kernel(
                 zero = small.tile([P, 1], F32, tag="zero", bufs=3)
                 nc.vector.memset(zero[:], 0.0)
                 zeros[tick + 2] = zero
+            if tick == -14:
+                transpose_misc()
+                keep_clip()
             if -14 <= tick <= -13:
                 h = tick + 14
                 regroup_w("g", h, 0, "u", 4)
                 regroup_w("g", h, 1, "u", 4)
                 quantize_w("g", h)
+            if tick == -13:
+                nc.scalar.activation(out=warm[:], in_=ones[:], func=ACT.Exp)
+                box_sizes()
+                box_floor()
+                box_inverse()
+                box_shift()

@@ -66,7 +66,7 @@ def tile_gaussianqueryassignment_t_kernel(
 
         def gpsimd_columns(j):
             g, b = blocks[j]
-            return 0 if g == final else (D, D // 2, D, 0)[b]
+            return 0 if g == final else (D, D, D, 0)[b]
 
         turns = {}
         for j, (g, b) in enumerate(blocks):
@@ -79,7 +79,7 @@ def tile_gaussianqueryassignment_t_kernel(
         for g, nb in enumerate(widths):
             f = first[g]
             e = last[g] if g < final else max(turns) - 1
-            lead = (16, 11, 12)[g] if g < 3 else 15
+            lead = (16, 11, 12)[g] if g < 3 else 14
             at["t0a"][f - lead] = g
             at["eva"][f - lead + 1] = g
             at["q0"][f - (13 if g == 0 else 9)] = g
@@ -90,9 +90,12 @@ def tile_gaussianqueryassignment_t_kernel(
                 at["load_x"][f - 26] = g
                 if g > 0:
                     at["load_cen"][f - 8] = g
-                at["t0b"][f - lead + 1] = g
-                at["evb"][f - lead + 2] = g
+                second = f - lead + 2 if g < 3 else f - 10
+                at["t0b"][second - 1] = g
+                at["evb"][second] = g
                 gate = (f + 1, f + 2, f + 3, f + 4) if g > 0 else (-8, -8, -8, -6)
+                if g == final:
+                    gate = (f, f + 1, f + 2, f + 3)
                 for kind, tick in zip(("abs0", "abs1", "abs2", "gmax"), gate):
                     at[kind][tick] = g
                 at["s2"][e + 4 + late] = g
@@ -336,7 +339,7 @@ def tile_gaussianqueryassignment_t_kernel(
             if half == 0:
                 grouped = work.tile([P, widths[g] * G], BF16, align_bytes=64, tag="g0")
                 g0s[g] = grouped
-            word_copy(0 if half == 1 and g % 2 == 0 else 1, g0s[g], 2 * half, xts[g, half])
+            word_copy(1 - half, g0s[g], 2 * half, xts[g, half])
 
         def q0(g):
             codes = work.tile([P, widths[g] * P], U32, align_bytes=64, tag="codes0", bufs=3)
@@ -460,7 +463,10 @@ def tile_gaussianqueryassignment_t_kernel(
 
         def s2(g):
             t = frame_of(g)
-            sim = psum.tile([P, SB], F32, tag="ep")
+            if g == final:
+                sim = psum.tile([P, SB], F32, tag="u", bufs=4)
+            else:
+                sim = psum.tile([P, SB], F32, tag="ep")
             for h in range(2):
                 qc = slice(h * T * M + t * M, h * T * M + t * M + M)
                 nc.tensor.matmul_mx(
@@ -498,7 +504,10 @@ def tile_gaussianqueryassignment_t_kernel(
                     sums[:, 0, j:j + 1], lhsT=es[g][:, P * j:P * j + P], rhs=ones[:], start=False, stop=(j == 3)
                 )
             esums[g] = sums
-            e_t = psum.tile([P, 4, P], F32, tag="ep")
+            if g == final:
+                e_t = psum.tile([P, 4, P], F32, tag="u", bufs=4)
+            else:
+                e_t = psum.tile([P, 4, P], F32, tag="ep")
             for j in range(4):
                 nc.tensor.transpose(e_t[:, j, :], es[g][:, P * j:P * j + P], ident_f[:])
             ets[g] = e_t
@@ -542,11 +551,17 @@ def tile_gaussianqueryassignment_t_kernel(
             g = at["load_cen"].get(tick)
             if g is not None:
                 load_cen(g)
-            if is_block(tick + 8):
-                s1(tick + 8)
             g = at["s2"].get(tick)
             if g is not None:
                 s2(g)
+            if is_block(tick + 8):
+                s1(tick + 8)
+            g = at["q0"].get(tick)
+            if g is not None:
+                q0(g)
+            g = at["gmax"].get(tick)
+            if g is not None:
+                gate_max_a(g)
             if is_block(tick + 7):
                 add_bias(tick + 7, 0)
             g = at["t2"].get(tick)
@@ -554,14 +569,14 @@ def tile_gaussianqueryassignment_t_kernel(
                 inverse_total(g)
             if is_block(tick + 7):
                 add_bias(tick + 7, 1)
-            g = at["gmax"].get(tick)
-            if g is not None:
-                gate_max_a(g)
             g = at["exp"].get(tick)
             if g is not None:
                 expo(g)
             if is_block(tick + 6):
                 square(tick + 6)
+            g = at["evb"].get(tick)
+            if g is not None:
+                t0_evac(g, 1)
             g = at["q2"].get(tick)
             if g is not None:
                 q2(g)
@@ -592,9 +607,6 @@ def tile_gaussianqueryassignment_t_kernel(
             g = at["eva"].get(tick)
             if g is not None:
                 t0_evac(g, 0)
-            g = at["evb"].get(tick)
-            if g is not None:
-                t0_evac(g, 1)
             for c in range(3):
                 g = at["abs%d" % c].get(tick)
                 if g is not None:
@@ -605,9 +617,6 @@ def tile_gaussianqueryassignment_t_kernel(
             g = at["t2"].get(tick)
             if g is not None:
                 finish(g)
-            g = at["q0"].get(tick)
-            if g is not None:
-                q0(g)
             if is_block(tick + 2) and gpsimd_columns(tick + 2) > 0:
                 zero = small.tile([P, 1], F32, tag="zero", bufs=3)
                 nc.vector.memset(zero[:], 0.0)

from contextlib import ExitStack

import concourse.mybir as mybir
from concourse.masks import make_identity

F32 = mybir.dt.float32
BF16 = mybir.dt.bfloat16
U32 = mybir.dt.uint32
U8 = mybir.dt.uint8
FP8X4 = mybir.dt.float8_e4m3fn_x4
ALU = mybir.AluOpType
ACT = mybir.ActivationFunctionType
AX = mybir.AxisListType

P = 128
T = 2
N = 4096
M = 128
A_W = 384
G = 512
D = 1024
SB = 512
NSB = T * N // SB
FLOPS = 2 * (T * N * G * D + T * N * D * M + T * M * G * D)
QUERIES = 1


def tile_gaussianqueryassignment_t_kernel(
    tc, center, instance_affinity, motion_code, keep_score, query_box3d, query_feat,
    presence_logit, Wq, bq, Wg, bg, background_bias, out,
):
    nc = tc.nc
    with ExitStack() as ctx:
        ctx.enter_context(tc.manual_schedule())
        const = ctx.enter_context(tc.tile_pool(name="const", bufs=1))
        setup = ctx.enter_context(tc.tile_pool(name="setup", bufs=1))
        xpool = ctx.enter_context(tc.tile_pool(name="xpool", bufs=5))
        work = ctx.enter_context(tc.tile_pool(name="work", bufs=2))
        vpool = ctx.enter_context(tc.tile_pool(name="vpool", bufs=8))
        small = ctx.enter_context(tc.tile_pool(name="small", bufs=6))
        epool = ctx.enter_context(tc.tile_pool(name="epool", bufs=2))
        opool = ctx.enter_context(tc.tile_pool(name="opool", bufs=3))
        psum = ctx.enter_context(tc.psum_pool(name="psum", bufs=1))

        widths = [4] * (NSB + 1)
        widths[QUERIES] = T
        blocks = []
        first = []
        last = []
        for g, nb in enumerate(widths):
            first.append(len(blocks))
            for b in range(nb):
                blocks.append((g, b))
            last.append(len(blocks) - 1)
        nblocks = len(blocks)
        final = len(widths) - 1

        def sb_of(g):
            return g if g < QUERIES else g - 1

        def frame_of(g):
            return sb_of(g) // (NSB // T)

        def n0_of(g):
            return SB * (sb_of(g) % (NSB // T))

        def gpsimd_columns(j):
            g, b = blocks[j]
            return 0 if g == final else (D, D, D, 0)[b]

        turns = {}
        for j, (g, b) in enumerate(blocks):
            turns.setdefault(j if g < final else first[g] + b // 2, []).append(j)

        at = {}
        for kind in ("load_x", "load_cen", "t0a", "eva", "t0b", "evb", "q0", "rn", "abs0", "abs1", "abs2",
                     "gmax", "q2", "s2", "exp", "t2"):
            at[kind] = {}
        for g, nb in enumerate(widths):
            f = first[g]
            e = last[g] if g < final else max(turns) - 1
            lead = (16, 11, 12)[g] if g < 3 else 14
            at["t0a"][f - lead] = g
            at["eva"][f - lead + 1] = g
            at["q0"][f - (13 if g == 0 else 9)] = g
            at["rn"][f - 3] = g
            at["q2"][e + 3] = g
            if g != QUERIES:
                late = 2 if g < QUERIES else 0
                at["load_x"][f - 26] = g
                if g > 0:
                    at["load_cen"][f - 8] = g
                second = f - lead + 2 if g < 3 else f - 10
                at["t0b"][second - 1] = g
                at["evb"][second] = g
                gate = (f + 1, f + 2, f + 3, f + 4) if g > 0 else (-8, -8, -8, -6)
                if g == final:
                    gate = (f, f + 1, f + 2, f + 3)
                for kind, tick in zip(("abs0", "abs1", "abs2", "gmax"), gate):
                    at[kind][tick] = g
                at["s2"][e + 4 + late] = g
                at["exp"][e + 5 + late] = g
                at["t2"][e + 6 + late] = g

        ident_f = const.tile([P, P], F32)
        make_identity(nc, ident_f[:])
        ident_b = const.tile([P, P], BF16)
        make_identity(nc, ident_b[:])
        neg_half = const.tile([P, 4], F32)
        nc.vector.memset(neg_half[:], -0.5)
        ones = const.tile([P, 1], F32)
        nc.vector.memset(ones[:], 1.0)

        misc = setup.tile([P, P], BF16)
        nc.vector.memset(misc[:], 0.0)
        pres_b = setup.tile([P, T * M], BF16)
        box = setup.tile([P, T, 7], BF16)
        bgb = setup.tile([P, 1], BF16)
        bg_b = const.tile([P, D], BF16)
        bq_b = const.tile([P, D], BF16)
        warm = setup.tile([P, 1], F32)
        nc.scalar.activation(out=warm[:], in_=ones[:], func=ACT.Ln)

        def load_keep():
            nc.sync.dma_start(
                out=misc[0:64, :], in_=keep_score[0].rearrange("t (b p) -> (t b) p", p=P)
            )
            nc.sync.dma_start(out=misc[64:66, :], in_=presence_logit[0])

        def load_small():
            nc.sync.dma_start(
                out=pres_b[:], in_=presence_logit[0].rearrange("t m -> (t m)").partition_broadcast(P)
            )
            nc.sync.dma_start(out=bgb[:], in_=background_bias.partition_broadcast(P))
            nc.sync.dma_start(out=bq_b[:], in_=bq.partition_broadcast(P))

        q_raw = setup.tile([P, T * G], BF16)

        def copy_out(which, out_ap, in_ap):
            if which == 0:
                nc.vector.tensor_copy(out=out_ap, in_=in_ap)
            else:
                nc.scalar.copy(out=out_ap, in_=in_ap)

        def word_transposes(words, b0, tag, bufs):
            xt = psum.tile([P, 2, 2, P], F32, tag=tag, bufs=bufs)
            for b in range(2):
                for u in range(2):
                    c0 = (b0 + b) * 256 + P * u
                    nc.tensor.transpose(xt[:, b, u, :], words[:, c0:c0 + P], ident_f[:])
            return xt

        def word_copy(which, grouped, b0, xt):
            g32 = grouped[:].bitcast(F32).rearrange("p (b r u) -> p b r u", r=P, u=2)
            copy_out(which, g32[:, b0:b0 + 2], xt[:].rearrange("p b u r -> p b r u"))

        w_raws = {}
        w_codes = {}
        w_scales = {}

        def load_w(name, w):
            raw = setup.tile([P, 8 * G], BF16, tag="w_raw", bufs=2)
            rv = raw[:].rearrange("p (a k) -> p a k", k=G)
            wv = w.rearrange("(a p) k -> p a k", p=P)
            for h in range(2):
                nc.sync.dma_start(out=rv[:, 4 * h:4 * h + 4, :], in_=wv[:, 4 * h:4 * h + 4, :])
            w_raws[name] = raw
            w_codes[name] = const.tile([P, D], U32, align_bytes=64, name="w_codes_" + name)
            w_scales[name] = const.tile([P, D], U8, align_bytes=64, name="w_scales_" + name)

        grouped_ws = {}

        def regroup_w(name, h, i, tag, bufs):
            if i == 0:
                grouped_w = setup.tile([P, 4 * G], BF16, align_bytes=64, tag="g0w", bufs=2)
                grouped_ws[name, h] = grouped_w
            xt = word_transposes(w_raws[name][:].bitcast(F32), 4 * h + 2 * i, tag, bufs)
            word_copy(i, grouped_ws[name, h], 2 * i, xt)

        def quantize_w(name, h):
            dcols = slice(512 * h, 512 * h + 512)
            nc.vector.quantize_mx(
                out=w_codes[name][:, dcols].bitcast(FP8X4), scales=w_scales[name][:, dcols],
                in_=grouped_ws[name, h][:],
            )

        q_codes = const.tile([P, 2 * T * M], U32, align_bytes=64)
        q_scales = const.tile([P, 2 * T * M], U8, align_bytes=64)

        a6 = const.tile([P, T, 3], F32)
        nqa6 = const.tile([P, T, 3], F32)
        bias_p = const.tile([P, T], F32)
        ebg = const.tile([P, 64], F32)
        pmax = setup.tile([P, T], F32)
        ks = setup.tile([P, 64], F32)
        l1 = setup.tile([P, 64], F32)
        l2 = setup.tile([P, 64], F32)

        misc_ts = []
        sizes = []

        def transpose_misc():
            misc_t = psum.tile([P, P], BF16, tag="ep")
            nc.tensor.transpose(misc_t[:], misc[:], ident_b[:])
            misc_ts.append(misc_t)

        def box_sizes():
            size = setup.tile([P, T, 3], F32)
            nc.vector.scalar_tensor_tensor(
                out=size[:], in0=box[:, :, 3:6], scalar=-1.0, in1=box[:, :, 3:6], op0=ALU.mult, op1=ALU.max
            )
            sizes.append(size)

        def box_floor():
            nc.vector.tensor_scalar(
                out=sizes[0][:], in0=sizes[0][:], scalar1=0.5, scalar2=1.5, op0=ALU.max, op1=ALU.mult
            )

        def box_inverse():
            nc.vector.reciprocal(out=a6[:], in_=sizes[0][:])

        def box_shift():
            nc.vector.scalar_tensor_tensor(
                out=nqa6[:], in0=box[:, :, 0:3], scalar=-1.0, in1=a6[:], op0=ALU.mult, op1=ALU.mult
            )

        def presence_max():
            nc.vector.tensor_reduce(
                out=pmax[:], in_=pres_b[:].rearrange("p (t m) -> p t m", m=M), axis=AX.X, op=ALU.max
            )

        def keep_clip():
            nc.vector.tensor_scalar(
                out=ks[:], in0=misc_ts[0][:, 0:64], scalar1=1e-4, scalar2=1.0 - 1e-4, op0=ALU.max, op1=ALU.min
            )
            nc.scalar.activation(out=l1[:], in_=ks[:], func=ACT.Ln)
            nc.scalar.activation(out=l2[:], in_=ks[:], func=ACT.Ln, scale=-1.0, bias=1.0)

        def query_bias():
            nc.vector.scalar_tensor_tensor(
                out=bias_p[:], in0=misc_ts[0][:, 64:66], scalar=-6.0, in1=pmax[:], op0=ALU.add, op1=ALU.subtract
            )

        dl = setup.tile([P, 64], F32)
        bgb9 = setup.tile([P, 1], F32)
        cb = setup.tile([P, T], F32)
        lb = setup.tile([P, 64], F32)

        def background_shift():
            nc.vector.tensor_scalar_add(out=bgb9[:], in0=bgb[:], scalar1=-9.0)

        def background_bias_of_frames():
            nc.vector.tensor_scalar(
                out=cb[:], in0=pmax[:], scalar1=-1.0, scalar2=bgb9[:, 0:1], op0=ALU.mult, op1=ALU.add
            )

        def log_odds():
            nc.vector.tensor_tensor(out=dl[:], in0=l1[:], in1=l2[:], op=ALU.subtract)

        def background_logits():
            for t in range(T):
                nc.vector.tensor_scalar(
                    out=lb[:, 32 * t:32 * t + 32], in0=dl[:, 32 * t:32 * t + 32],
                    scalar1=-0.5, scalar2=cb[:, t:t + 1], op0=ALU.mult, op1=ALU.add,
                )

        def background_exp():
            nc.vector.tensor_scalar_min(out=lb[:], in0=lb[:], scalar1=80.0)
            nc.scalar.activation(out=ebg[:], in_=lb[:], func=ACT.Exp)

        chores = [
            lambda: regroup_w("q", 0, 0, "tt", 3),
            lambda: regroup_w("q", 0, 1, "tt", 3),
            lambda: quantize_w("q", 0),
            lambda: regroup_w("q", 1, 0, "tt", 3),
            lambda: regroup_w("q", 1, 1, "tt", 3),
            lambda: quantize_w("q", 1),
            presence_max,
            query_bias,
            background_shift,
            background_bias_of_frames,
            log_odds,
            background_logits,
            background_exp,
        ]

        words = {QUERIES: q_raw[:].bitcast(F32)}
        cens = {}
        xts = {}
        g0s = {}
        codes0 = {}
        scales0 = {}
        us = {}
        vs = {}
        sss = {}
        rns = {}
        zeros = {}
        gfbs = {}
        t1s = {}
        g2s = {}
        codes2 = {QUERIES: q_codes}
        scales2 = {QUERIES: q_scales}
        dists = {}
        m1s = {}
        m2s = {}
        rts = {}
        sims = {}
        ys = {}
        es = {}
        ets = {}
        esums = {}

        def load_x(g):
            t = frame_of(g)
            n0 = n0_of(g)
            x = xpool.tile([P, 4 * G], BF16, tag="x")
            xv = x[:].rearrange("p (b k) -> p b k", k=G)
            nc.sync.dma_start(
                out=xv[:, :, 0:A_W],
                in_=instance_affinity[0, t, n0:n0 + SB, :].rearrange("(b p) k -> p b k", p=P),
            )
            nc.sync.dma_start(
                out=xv[:, :, A_W:G],
                in_=motion_code[0, t, n0:n0 + SB, :].rearrange("(b p) k -> p b k", p=P),
            )
            words[g] = x[:].bitcast(F32)

        def load_cen(g):
            t = frame_of(g)
            n0 = n0_of(g)
            cen = epool.tile([P, 3 * SB], BF16, tag="cen", bufs=3)
            nc.sync.dma_start(out=cen[:], in_=center[0, t, 3 * n0:3 * n0 + 3 * SB].partition_broadcast(P))
            cens[g] = cen

        def t0(g, half):
            xts[g, half] = word_transposes(words[g], 2 * half, "tt", 3)

        def t0_evac(g, half):
            if half == 0:
                grouped = work.tile([P, widths[g] * G], BF16, align_bytes=64, tag="g0")
                g0s[g] = grouped
            word_copy(1 - half, g0s[g], 2 * half, xts[g, half])

        def q0(g):
            codes = work.tile([P, widths[g] * P], U32, align_bytes=64, tag="codes0", bufs=3)
            scales = work.tile([P, widths[g] * P], U8, align_bytes=64, tag="scales0", bufs=3)
            nc.vector.quantize_mx(out=codes[:].bitcast(FP8X4), scales=scales[:], in_=g0s[g][:])
            codes0[g] = codes
            scales0[g] = scales

        def s1(j):
            g, b = blocks[j]
            name = "q" if g == QUERIES else "g"
            cols = slice(P * b, P * b + P)
            us[j] = []
            for h in range(2):
                dcols = slice(512 * h, 512 * h + 512)
                u = psum.tile([P, 512], F32, tag="u", bufs=4)
                nc.tensor.matmul_mx(
                    out=u[:],
                    lhsT=codes0[g][:, cols].bitcast(FP8X4),
                    lhsT_scale=scales0[g][:, cols],
                    rhs=w_codes[name][:, dcols].bitcast(FP8X4),
                    rhs_scale=w_scales[name][:, dcols],
                    start=True,
                    stop=True,
                )
                us[j].append(u)

        def add_bias(j, h):
            g, b = blocks[j]
            bias_b = bq_b if g == QUERIES else bg_b
            if h == 0:
                v = vpool.tile([P, D], F32, tag="v")
                vs[j] = v
            dcols = slice(512 * h, 512 * h + 512)
            nc.vector.tensor_tensor(out=vs[j][:, dcols], in0=us[j][h][:], in1=bias_b[:, dcols], op=ALU.add)

        def square(j):
            g, b = blocks[j]
            if b == 0:
                ss = small.tile([P, 4], F32, tag="ss", bufs=3)
                sss[g] = ss
            junk = work.tile([P, D], BF16, tag="junk", bufs=1)
            nc.scalar.activation(out=junk[:], in_=vs[j][:], func=ACT.Square, accum_out=sss[g][:, b:b + 1])

        def inverse_norms(g):
            nb = widths[g]
            ssc = small.tile([P, 4], F32, tag="ssc", bufs=2)
            nc.gpsimd.tensor_scalar(out=ssc[:, 0:nb], in0=sss[g][:, 0:nb], scalar1=1e-24, scalar2=None, op0=ALU.max)
            rn = small.tile([P, 4], F32, tag="rn", bufs=3)
            nc.gpsimd.tensor_tensor(out=rn[:, 0:nb], in0=ssc[:, 0:nb], in1=neg_half[:, 0:nb], op=ALU.pow)
            rns[g] = rn

        def scale(j):
            g, b = blocks[j]
            gfb = work.tile([P, D], BF16, tag="gfb", bufs=4)
            share = gpsimd_columns(j)
            if share > 0:
                nc.gpsimd.tensor_scalar(
                    out=gfb[:, 0:share], in0=vs[j][:, 0:share], scalar1=rns[g][:, b:b + 1],
                    scalar2=zeros[j][:, 0:1], op0=ALU.mult, op1=ALU.add,
                )
            if share < D:
                nc.vector.tensor_scalar_mul(
                    out=gfb[:, share:D], in0=vs[j][:, share:D], scalar1=rns[g][:, b:b + 1]
                )
            gfbs[j] = gfb

        def t1(j):
            words_j = gfbs[j][:].bitcast(F32)
            tt = psum.tile([P, 2, 2, P], F32, tag="tt", bufs=3)
            for h in range(2):
                for u in range(2):
                    c0 = P * (2 * h + u)
                    nc.tensor.transpose(tt[:, h, u, :], words_j[:, c0:c0 + P], ident_f[:])
            t1s[j] = tt

        def t1_evac(j):
            g, b = blocks[j]
            if b == 0:
                grouped = work.tile([P, 2, widths[g] * P, 4], BF16, align_bytes=64, tag="grouped2")
                g2s[g] = grouped
            copy_out(
                1,
                g2s[g][:].bitcast(F32)[:, :, P * b:P * b + P, :],
                t1s[j][:].rearrange("p h u n -> p h n u"),
            )

        def q2(g):
            if g != QUERIES:
                codes = work.tile([P, 2 * SB], U32, align_bytes=64, tag="codes2")
                scales = work.tile([P, 2 * SB], U8, align_bytes=64, tag="scales2")
                codes2[g] = codes
                scales2[g] = scales
            nc.vector.quantize_mx(
                out=codes2[g][:].bitcast(FP8X4),
                scales=scales2[g][:],
                in_=g2s[g][:].rearrange("p g n t -> p (g n t)"),
            )

        def gate_abs(g, c):
            t = frame_of(g)
            if c == 0:
                dist = epool.tile([P, 3, SB], F32, tag="dist")
                dists[g] = dist
            cv = cens[g][:].rearrange("p (n c) -> p n c", c=3)
            nc.scalar.activation(
                out=dists[g][:, c, :], in_=cv[:, :, c], func=ACT.Abs,
                scale=a6[:, t, c:c + 1], bias=nqa6[:, t, c:c + 1],
            )

        def gate_max_a(g):
            dist = dists[g]
            m1 = epool.tile([P, SB], F32, tag="m1")
            nc.vector.tensor_tensor(out=m1[:], in0=dist[:, 0, :], in1=dist[:, 1, :], op=ALU.max)
            m1s[g] = m1

        def gate_max_b(g):
            m2 = epool.tile([P, SB], F32, tag="m2", bufs=4)
            nc.vector.tensor_tensor(out=m2[:], in0=m1s[g][:], in1=dists[g][:, 2, :], op=ALU.max)
            m2s[g] = m2

        def s2(g):
            t = frame_of(g)
            if g == final:
                sim = psum.tile([P, SB], F32, tag="u", bufs=4)
            else:
                sim = psum.tile([P, SB], F32, tag="ep")
            for h in range(2):
                qc = slice(h * T * M + t * M, h * T * M + t * M + M)
                nc.tensor.matmul_mx(
                    out=sim[:],
                    lhsT=q_codes[:, qc].bitcast(FP8X4),
                    lhsT_scale=q_scales[:, qc],
                    rhs=codes2[g][:, h * SB:h * SB + SB].bitcast(FP8X4),
                    rhs_scale=scales2[g][:, h * SB:h * SB + SB],
                    start=(h == 0),
                    stop=(h == 1),
                )
            sims[g] = sim

        def logits(g):
            y = epool.tile([P, SB], F32, tag="y")
            nc.vector.scalar_tensor_tensor(
                out=y[:], in0=m2s[g][:], scalar=11.0 / 6.0, in1=sims[g][:], op0=ALU.min, op1=ALU.subtract
            )
            ys[g] = y

        def expo(g):
            t = frame_of(g)
            e = epool.tile([P, SB], F32, tag="e")
            nc.scalar.activation(out=e[:], in_=ys[g][:], func=ACT.Exp, scale=-6.0, bias=bias_p[:, t:t + 1])
            es[g] = e

        def t2(g):
            bc = slice(4 * sb_of(g), 4 * sb_of(g) + 4)
            sums = psum.tile([P, 2, 4], F32, tag="tt", bufs=3)
            nc.tensor.matmul(
                sums[:], lhsT=ident_f[:], rhs=ebg[:, bc].unsqueeze(1).to_broadcast([P, 2, 4]), start=True, stop=False
            )
            for j in range(4):
                nc.tensor.matmul(
                    sums[:, 0, j:j + 1], lhsT=es[g][:, P * j:P * j + P], rhs=ones[:], start=False, stop=(j == 3)
                )
            esums[g] = sums
            if g == final:
                e_t = psum.tile([P, 4, P], F32, tag="u", bufs=4)
            else:
                e_t = psum.tile([P, 4, P], F32, tag="ep")
            for j in range(4):
                nc.tensor.transpose(e_t[:, j, :], es[g][:, P * j:P * j + P], ident_f[:])
            ets[g] = e_t

        def inverse_total(g):
            rt = small.tile([P, 4], F32, tag="rt")
            nc.vector.reciprocal(out=rt[:], in_=esums[g][:, 0, :])
            rts[g] = rt

        def finish(g):
            s = sb_of(g)
            e_t = ets[g]
            rt = rts[g]
            o = opool.tile([P, 4, M + 1], F32, tag="o")
            nc.vector.tensor_tensor(
                out=o[:, :, 1:M + 1], in0=e_t[:], in1=rt[:].unsqueeze(2).to_broadcast([P, 4, M]), op=ALU.mult
            )
            nc.vector.tensor_tensor(out=o[:, :, 0], in0=esums[g][:, 1, :], in1=rt[:], op=ALU.mult)
            nc.sync.dma_start(
                out=out[0, SB * s:SB * s + SB, :].rearrange("(j p) c -> p j c", p=P), in_=o[:]
            )

        def is_block(j):
            return 0 <= j < nblocks

        for tick in range(-26, nblocks + 7):
            g = at["load_x"].get(tick)
            if g is not None:
                load_x(g)
            if tick == -26:
                load_keep()
                load_w("g", Wg)
                nc.sync.dma_start(out=box[:], in_=query_box3d[0].rearrange("t m c -> m t c"))
                nc.sync.dma_start(out=bg_b[:], in_=bg.partition_broadcast(P))
                load_cen(0)
                nc.sync.dma_start(
                    out=q_raw[:].rearrange("p (t k) -> p t k", k=G), in_=query_feat[0].rearrange("t m k -> m t k")
                )
                load_w("q", Wq)
                load_small()
            g = at["load_cen"].get(tick)
            if g is not None:
                load_cen(g)
            g = at["s2"].get(tick)
            if g is not None:
                s2(g)
            if is_block(tick + 8):
                s1(tick + 8)
            g = at["q0"].get(tick)
            if g is not None:
                q0(g)
            g = at["gmax"].get(tick)
            if g is not None:
                gate_max_a(g)
            if is_block(tick + 7):
                add_bias(tick + 7, 0)
            g = at["t2"].get(tick)
            if g is not None:
                inverse_total(g)
            if is_block(tick + 7):
                add_bias(tick + 7, 1)
            g = at["exp"].get(tick)
            if g is not None:
                expo(g)
            if is_block(tick + 6):
                square(tick + 6)
            g = at["evb"].get(tick)
            if g is not None:
                t0_evac(g, 1)
            g = at["q2"].get(tick)
            if g is not None:
                q2(g)
            for j in turns.get(tick + 1, []):
                scale(j)
            g = at["gmax"].get(tick)
            if g is not None:
                gate_max_b(g)
            g = at["rn"].get(tick)
            if g is not None:
                inverse_norms(g)
            for step in chores[0:2] if tick >= -7 else []:
                step()
                chores.remove(step)
            for j in turns.get(tick, []):
                t1(j)
            g = at["t0a"].get(tick)
            if g is not None:
                t0(g, 0)
            g = at["t0b"].get(tick)
            if g is not None:
                t0(g, 1)
            g = at["exp"].get(tick)
            if g is not None:
                t2(g)
            for j in turns.get(tick - 1, []):
                t1_evac(j)
            g = at["eva"].get(tick)
            if g is not None:
                t0_evac(g, 0)
            for c in range(3):
                g = at["abs%d" % c].get(tick)
                if g is not None:
                    gate_abs(g, c)
            g = at["s2"].get(tick)
            if g is not None:
                logits(g)
            g = at["t2"].get(tick)
            if g is not None:
                finish(g)
            if is_block(tick + 2) and gpsimd_columns(tick + 2) > 0:
                zero = small.tile([P, 1], F32, tag="zero", bufs=3)
                nc.vector.memset(zero[:], 0.0)
                zeros[tick + 2] = zero
            if tick == -14:
                transpose_misc()
                keep_clip()
            if -14 <= tick <= -13:
                h = tick + 14
                regroup_w("g", h, 0, "u", 4)
                regroup_w("g", h, 1, "u", 4)
                quantize_w("g", h)
            if tick == -13:
                nc.scalar.activation(out=warm[:], in_=ones[:], func=ACT.Exp)
                box_sizes()
                box_floor()
                box_inverse()
                box_shift()
